import numpy as np
import ml_dtypes


def mxq(x, axis, fmt="e4m3"):
    dtype, down = {"e4m3": (ml_dtypes.float8_e4m3fn, 7), "e5m2": (ml_dtypes.float8_e5m2, 14)}[fmt]
    v = np.moveaxis(np.asarray(x, np.float32).astype(ml_dtypes.bfloat16).astype(np.float64), axis, -1)
    blocks = v.reshape(v.shape[:-1] + (-1, 32))
    amax = np.abs(blocks).max(-1, keepdims=True)
    byte = np.maximum(np.where(amax > 0, np.frexp(amax)[1] - 1 + 127, 0) - down, 1)
    scale = np.exp2(byte - 127.0)
    codes = (blocks / scale).astype(np.float32).astype(dtype).astype(np.float64)
    return np.moveaxis((codes * scale).reshape(v.shape), -1, axis)


WIDE = False


def mx_kscale(k):
    if not WIDE:
        return np.ones(k)
    levels = np.array([10, -10, 5, -5, 0])
    a = np.random.permutation(np.resize(levels, k // 512 * 4)).reshape(k // 512, 4)
    idx = np.arange(k)
    return np.exp2(a[idx // 512, idx % 128 // 32])


BF16 = ml_dtypes.bfloat16


def bf(x):
    return np.asarray(x, np.float32).astype(BF16)


def f64(x):
    return np.asarray(x).astype(np.float64)


N, TQ, TS, C, E = 4, 512, 1024, 1024, 1024
SQRT_HALF = np.sqrt(0.5)


def wn_weight(v, g):
    return g[:, None] * v / np.sqrt((v * v).sum(axis=1, keepdims=True))


def setup_inputs():
    t = mx_kscale(E)
    return {
        "x": bf(np.random.standard_normal((N, TQ, C))),
        "target_embedding": bf(np.random.standard_normal((N, TQ, E)) * t),
        "encoder_keys": bf(np.random.standard_normal((N, E, TS)) * 1.5 / np.sqrt(E) / t[:, None]),
        "in_proj_v": bf(np.random.standard_normal((E, C)) * (0.5 + np.random.random((E, 1))) / np.sqrt(C)),
        "in_proj_g": bf((1.0 + 0.1 * np.random.standard_normal(E)) * t),
        "in_proj_b": bf(0.2 * np.random.standard_normal(E) * t),
    }


def reference(x, target_embedding, encoder_keys, in_proj_v, in_proj_g, in_proj_b):
    wi = wn_weight(f64(in_proj_v), f64(in_proj_g))
    h = ((mxq(f64(x), 2, "e4m3") @ mxq(wi, 1, "e4m3").T) + f64(in_proj_b) + f64(target_embedding)) * SQRT_HALF
    return mxq(h, 2, "e4m3") @ mxq(f64(encoder_keys), 1, "e4m3")

@@ -1,0 +1,219 @@
+import math
+from contextlib import ExitStack
+
+import concourse.mybir as mybir
+from concourse.masks import make_identity
+
+F32 = mybir.dt.float32
+BF16 = mybir.dt.bfloat16
+U32 = mybir.dt.uint32
+U8 = mybir.dt.uint8
+FP8X4 = mybir.dt.float8_e4m3fn_x4
+ACT = mybir.ActivationFunctionType
+ALU = mybir.AluOpType
+
+P = 128
+PACK = 4
+K_PASS = P * PACK
+N_MOVE = 512
+
+BATCH, TQ, TS, C, E = 4, 512, 1024, 1024, 1024
+C_PASSES = C // K_PASS
+E_PASSES = E // K_PASS
+Q_TILES = TQ // P
+S_HALVES = TS // N_MOVE
+SQRT_HALF = math.sqrt(0.5)
+
+FLOPS = 2 * BATCH * TQ * C * E + 2 * BATCH * TQ * E * TS
+
+
+def tile_attentionlayer_pa_kernel(
+    tc, x, target_embedding, encoder_keys, in_proj_v, in_proj_g, in_proj_b, out
+):
+    nc = tc.nc
+    with ExitStack() as stack:
+        const = stack.enter_context(tc.tile_pool(name="const", bufs=1))
+        raw = stack.enter_context(tc.tile_pool(name="raw", bufs=2))
+        work = stack.enter_context(tc.tile_pool(name="work", bufs=2))
+        psum_t = stack.enter_context(tc.psum_pool(name="psum_t", bufs=3))
+        psum_h = stack.enter_context(tc.psum_pool(name="psum_h", bufs=3))
+        psum_o = stack.enter_context(tc.psum_pool(name="psum_o", bufs=2))
+
+        one = const.tile([P, 1], F32)
+        nc.vector.memset(one[:], 1.0)
+        warm = const.tile([P, 1], F32)
+        nc.scalar.activation(out=warm[:], in_=one[:], func=ACT.Sqrt)
+
+        ident_bf = const.tile([P, P], BF16)
+        make_identity(nc, ident_bf[:])
+        ident_f32 = const.tile([P, P], F32)
+        make_identity(nc, ident_f32[:])
+
+        e_tiles = E // P
+        gb_rows = const.tile([P, P], BF16)
+        nc.vector.memset(gb_rows[:], 0.0)
+        nc.scalar.dma_start(out=gb_rows[0:e_tiles, :], in_=in_proj_g.rearrange("(m p) -> m p", p=P))
+        nc.scalar.dma_start(
+            out=gb_rows[e_tiles : 2 * e_tiles, :], in_=in_proj_b.rearrange("(m p) -> m p", p=P)
+        )
+        gb_ps = psum_t.tile([P, P], BF16, tag="tp")
+        nc.tensor.transpose(gb_ps[:], gb_rows[:], ident_bf[:])
+        gain = const.tile([P, e_tiles], F32)
+        nc.vector.tensor_copy(out=gain[:], in_=gb_ps[:, 0:e_tiles])
+        bias_s = const.tile([P, e_tiles], F32)
+        nc.vector.tensor_scalar(
+            out=bias_s[:], in0=gb_ps[:, e_tiles : 2 * e_tiles], scalar1=SQRT_HALF, scalar2=None, op0=ALU.mult
+        )
+
+        w_codes = const.tile([P, E_PASSES, C_PASSES, K_PASS], U32, align_bytes=64)
+        w_scales = const.tile([P, E_PASSES, C_PASSES, K_PASS], U8, align_bytes=64)
+        for ge in range(E_PASSES):
+            v_sb = raw.tile([P, PACK, C], BF16)
+            for t in range(PACK):
+                row0 = K_PASS * ge + P * t
+                nc.sync.dma_start(out=v_sb[:, t, :], in_=in_proj_v[row0 : row0 + P, :])
+            sumsq = work.tile([P, PACK], F32)
+            for t in range(PACK):
+                squares = work.tile([P, C], BF16, bufs=1)
+                nc.scalar.activation(
+                    out=squares[:], in_=v_sb[:, t, :], func=ACT.Square, accum_out=sumsq[:, t : t + 1]
+                )
+            norm = work.tile([P, PACK], F32)
+            nc.scalar.activation(out=norm[:], in_=sumsq[:], func=ACT.Sqrt)
+            row_scale = work.tile([P, PACK], F32)
+            nc.vector.reciprocal(out=row_scale[:], in_=norm[:])
+            nc.vector.tensor_mul(out=row_scale[:], in0=row_scale[:], in1=gain[:, PACK * ge : PACK * ge + PACK])
+
+            w_grouped = work.tile([P, C_PASSES, K_PASS, PACK], BF16, align_bytes=64)
+            for t in range(PACK):
+                w_rows = work.tile([P, 2 * PACK, P], BF16, bufs=3)
+                nc.vector.tensor_scalar(
+                    out=w_rows[:].rearrange("p (j w) i -> p j w i", w=2),
+                    in0=v_sb[:, t, :].rearrange("p (j i w) -> p j w i", i=P, w=2),
+                    scalar1=row_scale[:, t : t + 1],
+                    scalar2=None,
+                    op0=ALU.mult,
+                )
+                w_ps = psum_t.tile([P, 2 * PACK, P], BF16, tag="tp")
+                for blk in range(2 * PACK):
+                    nc.tensor.transpose(w_ps[:, blk, :], w_rows[:, blk, :], ident_bf[:])
+                nc.scalar.copy(
+                    out=w_grouped[:, :, P * t : P * t + P, :],
+                    in_=w_ps[:].rearrange("p (g k) e -> p g e k", k=PACK),
+                )
+            nc.vector.quantize_mx(
+                out=w_codes[:, ge].rearrange("p g e -> p (g e)").bitcast(FP8X4),
+                scales=w_scales[:, ge].rearrange("p g e -> p (g e)"),
+                in_=w_grouped[:].rearrange("p g e k -> p (g e k)"),
+            )
+
+        for n in range(BATCH):
+            x_sb = raw.tile([P, Q_TILES, C], BF16)
+            nc.sync.dma_start(out=x_sb[:], in_=x[n].rearrange("(p r) c -> p r c", r=Q_TILES))
+            k_sb = raw.tile([P, E_PASSES, PACK, TS], BF16)
+            for ge in range(E_PASSES):
+                nc.sync.dma_start(
+                    out=k_sb[:, ge],
+                    in_=encoder_keys[n][K_PASS * ge : K_PASS * ge + K_PASS, :].rearrange("(t p) s -> p t s", p=P),
+                )
+            te_sb = raw.tile([P, Q_TILES, E], BF16)
+            nc.sync.dma_start(out=te_sb[:], in_=target_embedding[n].rearrange("(p r) e -> p r e", r=Q_TILES))
+
+            x_grouped = work.tile([P, C_PASSES * TQ * PACK], BF16, align_bytes=64)
+            x_words = x_grouped[:].bitcast(F32).rearrange("p (g q u) -> p g q u", g=C_PASSES, u=2)
+            for r in range(Q_TILES):
+                x_ps = psum_t.tile([P, 2 * C_PASSES, P], F32, tag="tp")
+                for j in range(2 * C_PASSES):
+                    nc.tensor.transpose(
+                        x_ps[:, j, :], x_sb[:, r, :].bitcast(F32)[:, P * j : P * j + P], ident_f32[:]
+                    )
+                nc.scalar.copy(
+                    out=x_words[:, :, P * r : P * r + P, :],
+                    in_=x_ps[:].rearrange("p (g u) q -> p g q u", u=2),
+                )
+            x_codes = work.tile([P, C_PASSES, TQ], U32, align_bytes=64)
+            x_scales = work.tile([P, C_PASSES, TQ], U8, align_bytes=64)
+            nc.vector.quantize_mx(
+                out=x_codes[:].rearrange("p g q -> p (g q)").bitcast(FP8X4),
+                scales=x_scales[:].rearrange("p g q -> p (g q)"),
+                in_=x_grouped[:],
+            )
+
+            k_codes = work.tile([P, E_PASSES, TS], U32, align_bytes=64)
+            k_scales = work.tile([P, E_PASSES, TS], U8, align_bytes=64)
+            for ge in range(E_PASSES):
+                for sh in range(S_HALVES):
+                    s_cols = slice(N_MOVE * sh, N_MOVE * sh + N_MOVE)
+                    k_grouped = work.tile([P, N_MOVE, PACK], BF16, align_bytes=64, bufs=3)
+                    nc.vector.tensor_copy(
+                        out=k_grouped[:].rearrange("p (c i) t -> p c t i", i=4),
+                        in_=k_sb[:, ge, :, s_cols].rearrange("p t (c i) -> p c t i", i=4),
+                    )
+                    nc.vector.quantize_mx(
+                        out=k_codes[:, ge, s_cols].bitcast(FP8X4),
+                        scales=k_scales[:, ge, s_cols],
+                        in_=k_grouped[:].rearrange("p s t -> p (s t)"),
+                    )
+
+            h_codes = work.tile([P, E_PASSES, TQ], U32, align_bytes=64)
+            h_scales = work.tile([P, E_PASSES, TQ], U8, align_bytes=64)
+            for ge in range(E_PASSES):
+                h_part = work.tile([P, PACK, TQ], F32)
+                for t in range(PACK):
+                    h_ps = psum_h.tile([P, TQ], F32)
+                    for gc in range(C_PASSES):
+                        nc.tensor.matmul_mx(
+                            out=h_ps[:],
+                            lhsT=w_codes[:, ge, gc, P * t : P * t + P].bitcast(FP8X4),
+                            lhsT_scale=w_scales[:, ge, gc, P * t : P * t + P],
+                            rhs=x_codes[:, gc, :].bitcast(FP8X4),
+                            rhs_scale=x_scales[:, gc, :],
+                            start=(gc == 0),
+                            stop=(gc == C_PASSES - 1),
+                        )
+                    m = PACK * ge + t
+                    nc.scalar.activation(
+                        out=h_part[:, t, :], in_=h_ps[:], func=ACT.Identity, bias=bias_s[:, m : m + 1], scale=SQRT_HALF
+                    )
+                h_grouped = work.tile([P, TQ, PACK], BF16, align_bytes=64)
+                for hq in range(2):
+                    q_cols = slice(2 * P * hq, 2 * P * hq + 2 * P)
+                    te_ps = psum_t.tile([P, PACK, 2 * P], BF16, tag="tp")
+                    for t in range(PACK):
+                        e0 = K_PASS * ge + P * t
+                        for rr in range(2):
+                            nc.tensor.transpose(
+                                te_ps[:, t, P * rr : P * rr + P], te_sb[:, 2 * hq + rr, e0 : e0 + P], ident_bf[:]
+                            )
+                    nc.vector.scalar_tensor_tensor(
+                        out=h_grouped[:, q_cols, :],
+                        in0=te_ps[:].rearrange("p t q -> p q t"),
+                        scalar=SQRT_HALF,
+                        in1=h_part[:, :, q_cols].rearrange("p t q -> p q t"),
+                        op0=ALU.mult,
+                        op1=ALU.add,
+                    )
+                nc.vector.quantize_mx(
+                    out=h_codes[:, ge, :].bitcast(FP8X4),
+                    scales=h_scales[:, ge, :],
+                    in_=h_grouped[:].rearrange("p q t -> p (q t)"),
+                )
+
+            out_rows = out[n].rearrange("(p r) s -> p r s", r=Q_TILES)
+            for r in range(Q_TILES):
+                o_sb = work.tile([P, TS], F32, bufs=4)
+                for sh in range(S_HALVES):
+                    s_cols = slice(N_MOVE * sh, N_MOVE * sh + N_MOVE)
+                    o_ps = psum_o.tile([P, N_MOVE], F32)
+                    for ge in range(E_PASSES):
+                        nc.tensor.matmul_mx(
+                            out=o_ps[:],
+                            lhsT=h_codes[:, ge, P * r : P * r + P].bitcast(FP8X4),
+                            lhsT_scale=h_scales[:, ge, P * r : P * r + P],
+                            rhs=k_codes[:, ge, s_cols].bitcast(FP8X4),
+                            rhs_scale=k_scales[:, ge, s_cols],
+                            start=(ge == 0),
+                            stop=(ge == E_PASSES - 1),
+                        )
+                    nc.scalar.copy(out=o_sb[:, s_cols], in_=o_ps[:])
+                nc.sync.dma_start(out=out_rows[:, r, :], in_=o_sb[:])

@@ -20,6 +20,7 @@ N_MOVE = 512
 BATCH, TQ, TS, C, E = 4, 512, 1024, 1024, 1024
 C_PASSES = C // K_PASS
 E_PASSES = E // K_PASS
+E_TILES = E // P
 Q_TILES = TQ // P
 S_HALVES = TS // N_MOVE
 SQRT_HALF = math.sqrt(0.5)
@@ -32,12 +33,233 @@ def tile_attentionlayer_pa_kernel(
 ):
     nc = tc.nc
     with ExitStack() as stack:
+        stack.enter_context(tc.manual_schedule())
         const = stack.enter_context(tc.tile_pool(name="const", bufs=1))
         raw = stack.enter_context(tc.tile_pool(name="raw", bufs=2))
         work = stack.enter_context(tc.tile_pool(name="work", bufs=2))
-        psum_t = stack.enter_context(tc.psum_pool(name="psum_t", bufs=3))
-        psum_h = stack.enter_context(tc.psum_pool(name="psum_h", bufs=3))
-        psum_o = stack.enter_context(tc.psum_pool(name="psum_o", bufs=2))
+        psum_t = stack.enter_context(tc.psum_pool(name="psum_t", bufs=4))
+        psum_mx = stack.enter_context(tc.psum_pool(name="psum_mx", bufs=4))
+
+        v_sb, sumsq, row_scale, w_rows, w_grouped = {}, {}, {}, {}, {}
+        x_sb, k_sb, te_sb = {}, {}, {}
+        x_grouped, x_codes, x_scales = {}, {}, {}
+        k_codes, k_scales = {}, {}
+        h_part, te_ps, h_codes, h_scales = {}, {}, {}, {}
+
+        def load_v(ge):
+            v_tile = raw.tile([P, PACK, C], BF16)
+            for t in range(PACK):
+                row0 = K_PASS * ge + P * t
+                nc.sync.dma_start(out=v_tile[:, t, :], in_=in_proj_v[row0 : row0 + P, :])
+            v_sb[ge] = v_tile
+
+        def load_batch(n):
+            x_tile = raw.tile([P, Q_TILES, C], BF16)
+            nc.sync.dma_start(out=x_tile[:], in_=x[n].rearrange("(p r) c -> p r c", r=Q_TILES))
+            x_sb[n] = x_tile
+            k_tile = raw.tile([P, E_PASSES, PACK, TS], BF16)
+            for ge in range(E_PASSES):
+                rows = encoder_keys[n][K_PASS * ge : K_PASS * ge + K_PASS, :]
+                nc.sync.dma_start(out=k_tile[:, ge], in_=rows.rearrange("(t p) s -> p t s", p=P))
+            k_sb[n] = k_tile
+            te_tile = raw.tile([P, Q_TILES, E], BF16)
+            nc.sync.dma_start(out=te_tile[:], in_=target_embedding[n].rearrange("(p r) e -> p r e", r=Q_TILES))
+            te_sb[n] = te_tile
+
+        def sum_squares(ge):
+            half = C // 2
+            sumsq_s = work.tile([P, PACK], F32)
+            sumsq_v = work.tile([P, PACK], F32)
+            for t in range(PACK):
+                squares_s = work.tile([P, half], BF16, bufs=1)
+                nc.scalar.activation(
+                    out=squares_s[:], in_=v_sb[ge][:, t, 0:half], func=ACT.Square, accum_out=sumsq_s[:, t : t + 1]
+                )
+                squares_v = work.tile([P, half], F32, bufs=1)
+                nc.vector.scalar_tensor_tensor(
+                    out=squares_v[:],
+                    in0=v_sb[ge][:, t, half:C],
+                    scalar=1.0,
+                    in1=v_sb[ge][:, t, half:C],
+                    op0=ALU.mult,
+                    op1=ALU.mult,
+                    accum_out=sumsq_v[:, t : t + 1],
+                )
+            sumsq[ge] = (sumsq_s, sumsq_v)
+
+        def row_scales(ge):
+            sumsq_s, sumsq_v = sumsq[ge]
+            total = work.tile([P, PACK], F32)
+            nc.vector.tensor_add(out=total[:], in0=sumsq_s[:], in1=sumsq_v[:])
+            norm = work.tile([P, PACK], F32)
+            nc.scalar.activation(out=norm[:], in_=total[:], func=ACT.Sqrt)
+            g_over_norm = work.tile([P, PACK], F32)
+            nc.vector.reciprocal(out=g_over_norm[:], in_=norm[:])
+            nc.vector.tensor_mul(out=g_over_norm[:], in0=g_over_norm[:], in1=gain[:, PACK * ge : PACK * ge + PACK])
+            row_scale[ge] = g_over_norm
+
+        def scale_rows(ge):
+            for t in range(PACK):
+                w_tile = work.tile([P, 2 * PACK, P], BF16, bufs=PACK)
+                nc.vector.tensor_scalar(
+                    out=w_tile[:].rearrange("p (j w) i -> p j w i", w=2),
+                    in0=v_sb[ge][:, t, :].rearrange("p (j i w) -> p j w i", i=P, w=2),
+                    scalar1=row_scale[ge][:, t : t + 1],
+                    scalar2=None,
+                    op0=ALU.mult,
+                )
+                w_rows[ge, t] = w_tile
+
+        def transpose_w(ge):
+            grouped = work.tile([P, C_PASSES, K_PASS, PACK], BF16, align_bytes=64, name="w_grouped")
+            for t in range(PACK):
+                w_ps = psum_t.tile([P, 2 * PACK, P], BF16, tag="tp")
+                for blk in range(2 * PACK):
+                    nc.tensor.transpose(w_ps[:, blk, :], w_rows[ge, t][:, blk, :], ident_bf[:])
+                nc.scalar.copy(
+                    out=grouped[:, :, P * t : P * t + P, :], in_=w_ps[:].rearrange("p (g k) e -> p g e k", k=PACK)
+                )
+            w_grouped[ge] = grouped
+
+        def quantise_w(ge):
+            nc.vector.quantize_mx(
+                out=w_codes[:, ge].rearrange("p g e -> p (g e)").bitcast(FP8X4),
+                scales=w_scales[:, ge].rearrange("p g e -> p (g e)"),
+                in_=w_grouped[ge][:].rearrange("p g e k -> p (g e k)"),
+            )
+
+        def transpose_x(n):
+            grouped = work.tile([P, C_PASSES * TQ * PACK], BF16, align_bytes=64, name="x_grouped")
+            words = grouped[:].bitcast(F32).rearrange("p (g q u) -> p g q u", g=C_PASSES, u=2)
+            for r in range(Q_TILES):
+                x_ps = psum_t.tile([P, 2 * C_PASSES, P], F32, tag="tp")
+                for j in range(2 * C_PASSES):
+                    nc.tensor.transpose(
+                        x_ps[:, j, :], x_sb[n][:, r, :].bitcast(F32)[:, P * j : P * j + P], ident_f32[:]
+                    )
+                nc.scalar.copy(
+                    out=words[:, :, P * r : P * r + P, :], in_=x_ps[:].rearrange("p (g u) q -> p g q u", u=2)
+                )
+            x_grouped[n] = grouped
+
+        def quantise_x(n):
+            codes = work.tile([P, C_PASSES, TQ], U32, align_bytes=64, name="x_codes")
+            scales = work.tile([P, C_PASSES, TQ], U8, align_bytes=64, name="x_scales")
+            nc.vector.quantize_mx(
+                out=codes[:].rearrange("p g q -> p (g q)").bitcast(FP8X4),
+                scales=scales[:].rearrange("p g q -> p (g q)"),
+                in_=x_grouped[n][:],
+            )
+            x_codes[n], x_scales[n] = codes, scales
+
+        def quantise_keys(n):
+            codes = work.tile([P, E_PASSES, TS], U32, align_bytes=64, name="k_codes")
+            scales = work.tile([P, E_PASSES, TS], U8, align_bytes=64, name="k_scales")
+            for ge in range(E_PASSES):
+                grouped = []
+                for sh in range(S_HALVES):
+                    k_grouped = work.tile([P, N_MOVE, PACK], BF16, align_bytes=64, bufs=3)
+                    nc.vector.tensor_copy(
+                        out=k_grouped[:].rearrange("p (c i) t -> p c t i", i=4),
+                        in_=k_sb[n][:, ge, :, N_MOVE * sh : N_MOVE * sh + N_MOVE].rearrange(
+                            "p t (c i) -> p c t i", i=4
+                        ),
+                    )
+                    grouped.append(k_grouped)
+                for sh in range(S_HALVES):
+                    s_cols = slice(N_MOVE * sh, N_MOVE * sh + N_MOVE)
+                    nc.vector.quantize_mx(
+                        out=codes[:, ge, s_cols].bitcast(FP8X4),
+                        scales=scales[:, ge, s_cols],
+                        in_=grouped[sh][:].rearrange("p s t -> p (s t)"),
+                    )
+            k_codes[n], k_scales[n] = codes, scales
+
+        def project(n):
+            for ge in range(E_PASSES):
+                part = work.tile([P, PACK, TQ], F32, name="h_part")
+                for t in range(PACK):
+                    h_ps = psum_mx.tile([P, TQ], F32, tag="mx")
+                    for gc in range(C_PASSES):
+                        nc.tensor.matmul_mx(
+                            out=h_ps[:],
+                            lhsT=w_codes[:, ge, gc, P * t : P * t + P].bitcast(FP8X4),
+                            lhsT_scale=w_scales[:, ge, gc, P * t : P * t + P],
+                            rhs=x_codes[n][:, gc, :].bitcast(FP8X4),
+                            rhs_scale=x_scales[n][:, gc, :],
+                            start=(gc == 0),
+                            stop=(gc == C_PASSES - 1),
+                        )
+                    m = PACK * ge + t
+                    nc.scalar.activation(
+                        out=part[:, t, :], in_=h_ps[:], func=ACT.Identity, bias=bias_s[:, m : m + 1], scale=SQRT_HALF
+                    )
+                h_part[n, ge] = part
+
+        def transpose_te(n):
+            for ge in range(E_PASSES):
+                for hq in range(2):
+                    bank = psum_t.tile([P, PACK, 2 * P], BF16, tag="tp", name="te_ps")
+                    for t in range(PACK):
+                        e0 = K_PASS * ge + P * t
+                        for rr in range(2):
+                            nc.tensor.transpose(
+                                bank[:, t, P * rr : P * rr + P], te_sb[n][:, 2 * hq + rr, e0 : e0 + P], ident_bf[:]
+                            )
+                    te_ps[n, ge, hq] = bank
+
+        def finish_h(n):
+            codes = work.tile([P, E_PASSES, TQ], U32, align_bytes=64, name="h_codes")
+            scales = work.tile([P, E_PASSES, TQ], U8, align_bytes=64, name="h_scales")
+            grouped = []
+            for ge in range(E_PASSES):
+                h_grouped = work.tile([P, TQ, PACK], BF16, align_bytes=64)
+                for hq in range(2):
+                    q_cols = slice(2 * P * hq, 2 * P * hq + 2 * P)
+                    nc.vector.scalar_tensor_tensor(
+                        out=h_grouped[:, q_cols, :],
+                        in0=te_ps[n, ge, hq][:].rearrange("p t q -> p q t"),
+                        scalar=SQRT_HALF,
+                        in1=h_part[n, ge][:, :, q_cols].rearrange("p t q -> p q t"),
+                        op0=ALU.mult,
+                        op1=ALU.add,
+                    )
+                grouped.append(h_grouped)
+            for ge in range(E_PASSES):
+                nc.vector.quantize_mx(
+                    out=codes[:, ge, :].bitcast(FP8X4),
+                    scales=scales[:, ge, :],
+                    in_=grouped[ge][:].rearrange("p q t -> p (q t)"),
+                )
+            h_codes[n], h_scales[n] = codes, scales
+
+        def scores(n, vector_helps):
+            out_rows = out[n].rearrange("(p r) s -> p r s", r=Q_TILES)
+            for r in range(Q_TILES):
+                o_sb = work.tile([P, TS], F32, bufs=4)
+                for sh in range(S_HALVES):
+                    s_cols = slice(N_MOVE * sh, N_MOVE * sh + N_MOVE)
+                    o_ps = psum_mx.tile([P, N_MOVE], F32, tag="mx")
+                    for ge in range(E_PASSES):
+                        nc.tensor.matmul_mx(
+                            out=o_ps[:],
+                            lhsT=h_codes[n][:, ge, P * r : P * r + P].bitcast(FP8X4),
+                            lhsT_scale=h_scales[n][:, ge, P * r : P * r + P],
+                            rhs=k_codes[n][:, ge, s_cols].bitcast(FP8X4),
+                            rhs_scale=k_scales[n][:, ge, s_cols],
+                            start=(ge == 0),
+                            stop=(ge == E_PASSES - 1),
+                        )
+                    if vector_helps and sh == 1:
+                        nc.vector.tensor_copy(out=o_sb[:, s_cols], in_=o_ps[:])
+                    else:
+                        nc.scalar.copy(out=o_sb[:, s_cols], in_=o_ps[:])
+                nc.sync.dma_start(out=out_rows[:, r, :], in_=o_sb[:])
+
+        for ge in range(E_PASSES):
+            load_v(ge)
+        load_batch(0)
+        load_batch(1)
 
         one = const.tile([P, 1], F32)
         nc.vector.memset(one[:], 1.0)
@@ -49,171 +271,53 @@ def tile_attentionlayer_pa_kernel(
         ident_f32 = const.tile([P, P], F32)
         make_identity(nc, ident_f32[:])
 
-        e_tiles = E // P
         gb_rows = const.tile([P, P], BF16)
         nc.vector.memset(gb_rows[:], 0.0)
-        nc.scalar.dma_start(out=gb_rows[0:e_tiles, :], in_=in_proj_g.rearrange("(m p) -> m p", p=P))
-        nc.scalar.dma_start(
-            out=gb_rows[e_tiles : 2 * e_tiles, :], in_=in_proj_b.rearrange("(m p) -> m p", p=P)
-        )
+        nc.scalar.dma_start(out=gb_rows[0:E_TILES, :], in_=in_proj_g.rearrange("(m p) -> m p", p=P))
+        nc.scalar.dma_start(out=gb_rows[E_TILES : 2 * E_TILES, :], in_=in_proj_b.rearrange("(m p) -> m p", p=P))
         gb_ps = psum_t.tile([P, P], BF16, tag="tp")
         nc.tensor.transpose(gb_ps[:], gb_rows[:], ident_bf[:])
-        gain = const.tile([P, e_tiles], F32)
-        nc.vector.tensor_copy(out=gain[:], in_=gb_ps[:, 0:e_tiles])
-        bias_s = const.tile([P, e_tiles], F32)
+        gain = const.tile([P, E_TILES], F32)
+        nc.vector.tensor_copy(out=gain[:], in_=gb_ps[:, 0:E_TILES])
+        bias_s = const.tile([P, E_TILES], F32)
         nc.vector.tensor_scalar(
-            out=bias_s[:], in0=gb_ps[:, e_tiles : 2 * e_tiles], scalar1=SQRT_HALF, scalar2=None, op0=ALU.mult
+            out=bias_s[:], in0=gb_ps[:, E_TILES : 2 * E_TILES], scalar1=SQRT_HALF, scalar2=None, op0=ALU.mult
         )
 
         w_codes = const.tile([P, E_PASSES, C_PASSES, K_PASS], U32, align_bytes=64)
         w_scales = const.tile([P, E_PASSES, C_PASSES, K_PASS], U8, align_bytes=64)
-        for ge in range(E_PASSES):
-            v_sb = raw.tile([P, PACK, C], BF16)
-            for t in range(PACK):
-                row0 = K_PASS * ge + P * t
-                nc.sync.dma_start(out=v_sb[:, t, :], in_=in_proj_v[row0 : row0 + P, :])
-            sumsq = work.tile([P, PACK], F32)
-            for t in range(PACK):
-                squares = work.tile([P, C], BF16, bufs=1)
-                nc.scalar.activation(
-                    out=squares[:], in_=v_sb[:, t, :], func=ACT.Square, accum_out=sumsq[:, t : t + 1]
-                )
-            norm = work.tile([P, PACK], F32)
-            nc.scalar.activation(out=norm[:], in_=sumsq[:], func=ACT.Sqrt)
-            row_scale = work.tile([P, PACK], F32)
-            nc.vector.reciprocal(out=row_scale[:], in_=norm[:])
-            nc.vector.tensor_mul(out=row_scale[:], in0=row_scale[:], in1=gain[:, PACK * ge : PACK * ge + PACK])
 
-            w_grouped = work.tile([P, C_PASSES, K_PASS, PACK], BF16, align_bytes=64)
-            for t in range(PACK):
-                w_rows = work.tile([P, 2 * PACK, P], BF16, bufs=3)
-                nc.vector.tensor_scalar(
-                    out=w_rows[:].rearrange("p (j w) i -> p j w i", w=2),
-                    in0=v_sb[:, t, :].rearrange("p (j i w) -> p j w i", i=P, w=2),
-                    scalar1=row_scale[:, t : t + 1],
-                    scalar2=None,
-                    op0=ALU.mult,
-                )
-                w_ps = psum_t.tile([P, 2 * PACK, P], BF16, tag="tp")
-                for blk in range(2 * PACK):
-                    nc.tensor.transpose(w_ps[:, blk, :], w_rows[:, blk, :], ident_bf[:])
-                nc.scalar.copy(
-                    out=w_grouped[:, :, P * t : P * t + P, :],
-                    in_=w_ps[:].rearrange("p (g k) e -> p g e k", k=PACK),
-                )
-            nc.vector.quantize_mx(
-                out=w_codes[:, ge].rearrange("p g e -> p (g e)").bitcast(FP8X4),
-                scales=w_scales[:, ge].rearrange("p g e -> p (g e)"),
-                in_=w_grouped[:].rearrange("p g e k -> p (g e k)"),
-            )
+        sum_squares(0)
+        row_scales(0)
+        scale_rows(0)
+        sum_squares(1)
+        transpose_w(0)
+        row_scales(1)
+        quantise_w(0)
+        scale_rows(1)
+        transpose_x(0)
+        transpose_w(1)
+        quantise_x(0)
+        quantise_w(1)
+        project(0)
+        transpose_x(1)
+        transpose_te(0)
+        quantise_keys(0)
+        quantise_x(1)
 
         for n in range(BATCH):
-            x_sb = raw.tile([P, Q_TILES, C], BF16)
-            nc.sync.dma_start(out=x_sb[:], in_=x[n].rearrange("(p r) c -> p r c", r=Q_TILES))
-            k_sb = raw.tile([P, E_PASSES, PACK, TS], BF16)
-            for ge in range(E_PASSES):
-                nc.sync.dma_start(
-                    out=k_sb[:, ge],
-                    in_=encoder_keys[n][K_PASS * ge : K_PASS * ge + K_PASS, :].rearrange("(t p) s -> p t s", p=P),
-                )
-            te_sb = raw.tile([P, Q_TILES, E], BF16)
-            nc.sync.dma_start(out=te_sb[:], in_=target_embedding[n].rearrange("(p r) e -> p r e", r=Q_TILES))
-
-            x_grouped = work.tile([P, C_PASSES * TQ * PACK], BF16, align_bytes=64)
-            x_words = x_grouped[:].bitcast(F32).rearrange("p (g q u) -> p g q u", g=C_PASSES, u=2)
-            for r in range(Q_TILES):
-                x_ps = psum_t.tile([P, 2 * C_PASSES, P], F32, tag="tp")
-                for j in range(2 * C_PASSES):
-                    nc.tensor.transpose(
-                        x_ps[:, j, :], x_sb[:, r, :].bitcast(F32)[:, P * j : P * j + P], ident_f32[:]
-                    )
-                nc.scalar.copy(
-                    out=x_words[:, :, P * r : P * r + P, :],
-                    in_=x_ps[:].rearrange("p (g u) q -> p g q u", u=2),
-                )
-            x_codes = work.tile([P, C_PASSES, TQ], U32, align_bytes=64)
-            x_scales = work.tile([P, C_PASSES, TQ], U8, align_bytes=64)
-            nc.vector.quantize_mx(
-                out=x_codes[:].rearrange("p g q -> p (g q)").bitcast(FP8X4),
-                scales=x_scales[:].rearrange("p g q -> p (g q)"),
-                in_=x_grouped[:],
-            )
-
-            k_codes = work.tile([P, E_PASSES, TS], U32, align_bytes=64)
-            k_scales = work.tile([P, E_PASSES, TS], U8, align_bytes=64)
-            for ge in range(E_PASSES):
-                for sh in range(S_HALVES):
-                    s_cols = slice(N_MOVE * sh, N_MOVE * sh + N_MOVE)
-                    k_grouped = work.tile([P, N_MOVE, PACK], BF16, align_bytes=64, bufs=3)
-                    nc.vector.tensor_copy(
-                        out=k_grouped[:].rearrange("p (c i) t -> p c t i", i=4),
-                        in_=k_sb[:, ge, :, s_cols].rearrange("p t (c i) -> p c t i", i=4),
-                    )
-                    nc.vector.quantize_mx(
-                        out=k_codes[:, ge, s_cols].bitcast(FP8X4),
-                        scales=k_scales[:, ge, s_cols],
-                        in_=k_grouped[:].rearrange("p s t -> p (s t)"),
-                    )
-
-            h_codes = work.tile([P, E_PASSES, TQ], U32, align_bytes=64)
-            h_scales = work.tile([P, E_PASSES, TQ], U8, align_bytes=64)
-            for ge in range(E_PASSES):
-                h_part = work.tile([P, PACK, TQ], F32)
-                for t in range(PACK):
-                    h_ps = psum_h.tile([P, TQ], F32)
-                    for gc in range(C_PASSES):
-                        nc.tensor.matmul_mx(
-                            out=h_ps[:],
-                            lhsT=w_codes[:, ge, gc, P * t : P * t + P].bitcast(FP8X4),
-                            lhsT_scale=w_scales[:, ge, gc, P * t : P * t + P],
-                            rhs=x_codes[:, gc, :].bitcast(FP8X4),
-                            rhs_scale=x_scales[:, gc, :],
-                            start=(gc == 0),
-                            stop=(gc == C_PASSES - 1),
-                        )
-                    m = PACK * ge + t
-                    nc.scalar.activation(
-                        out=h_part[:, t, :], in_=h_ps[:], func=ACT.Identity, bias=bias_s[:, m : m + 1], scale=SQRT_HALF
-                    )
-                h_grouped = work.tile([P, TQ, PACK], BF16, align_bytes=64)
-                for hq in range(2):
-                    q_cols = slice(2 * P * hq, 2 * P * hq + 2 * P)
-                    te_ps = psum_t.tile([P, PACK, 2 * P], BF16, tag="tp")
-                    for t in range(PACK):
-                        e0 = K_PASS * ge + P * t
-                        for rr in range(2):
-                            nc.tensor.transpose(
-                                te_ps[:, t, P * rr : P * rr + P], te_sb[:, 2 * hq + rr, e0 : e0 + P], ident_bf[:]
-                            )
-                    nc.vector.scalar_tensor_tensor(
-                        out=h_grouped[:, q_cols, :],
-                        in0=te_ps[:].rearrange("p t q -> p q t"),
-                        scalar=SQRT_HALF,
-                        in1=h_part[:, :, q_cols].rearrange("p t q -> p q t"),
-                        op0=ALU.mult,
-                        op1=ALU.add,
-                    )
-                nc.vector.quantize_mx(
-                    out=h_codes[:, ge, :].bitcast(FP8X4),
-                    scales=h_scales[:, ge, :],
-                    in_=h_grouped[:].rearrange("p q t -> p (q t)"),
-                )
-
-            out_rows = out[n].rearrange("(p r) s -> p r s", r=Q_TILES)
-            for r in range(Q_TILES):
-                o_sb = work.tile([P, TS], F32, bufs=4)
-                for sh in range(S_HALVES):
-                    s_cols = slice(N_MOVE * sh, N_MOVE * sh + N_MOVE)
-                    o_ps = psum_o.tile([P, N_MOVE], F32)
-                    for ge in range(E_PASSES):
-                        nc.tensor.matmul_mx(
-                            out=o_ps[:],
-                            lhsT=h_codes[:, ge, P * r : P * r + P].bitcast(FP8X4),
-                            lhsT_scale=h_scales[:, ge, P * r : P * r + P],
-                            rhs=k_codes[:, ge, s_cols].bitcast(FP8X4),
-                            rhs_scale=k_scales[:, ge, s_cols],
-                            start=(ge == 0),
-                            stop=(ge == E_PASSES - 1),
-                        )
-                    nc.scalar.copy(out=o_sb[:, s_cols], in_=o_ps[:])
-                nc.sync.dma_start(out=out_rows[:, r, :], in_=o_sb[:])
+            if n + 2 < BATCH:
+                load_batch(n + 2)
+            finish_h(n)
+            if n >= 1:
+                scores(n - 1, vector_helps=False)
+            if n + 1 < BATCH:
+                project(n + 1)
+            if n + 2 < BATCH:
+                transpose_x(n + 2)
+            if n + 1 < BATCH:
+                transpose_te(n + 1)
+                quantise_keys(n + 1)
+            if n + 2 < BATCH:
+                quantise_x(n + 2)
+        scores(BATCH - 1, vector_helps=True)

@@ -22,8 +22,10 @@ C_PASSES = C // K_PASS
 E_PASSES = E // K_PASS
 E_TILES = E // P
 Q_TILES = TQ // P
+Q_HALF = TQ // 2
 S_HALVES = TS // N_MOVE
 SQRT_HALF = math.sqrt(0.5)
+SCALAR_CHUNK = (1, 1)
 
 FLOPS = 2 * BATCH * TQ * C * E + 2 * BATCH * TQ * E * TS
 
@@ -40,10 +42,10 @@ def tile_attentionlayer_pa_kernel(
         psum_t = stack.enter_context(tc.psum_pool(name="psum_t", bufs=4))
         psum_mx = stack.enter_context(tc.psum_pool(name="psum_mx", bufs=4))
 
-        v_sb, sumsq, row_scale, w_rows, w_grouped = {}, {}, {}, {}, {}
+        v_sb, w_rows, w_grouped = {}, {}, {}
         x_sb, k_sb, te_sb = {}, {}, {}
         x_grouped, x_codes, x_scales = {}, {}, {}
-        k_codes, k_scales = {}, {}
+        k_from_scalar, k_codes, k_scales = {}, {}, {}
         h_part, te_ps, h_codes, h_scales = {}, {}, {}, {}
 
         def load_v(ge):
@@ -66,45 +68,44 @@ def tile_attentionlayer_pa_kernel(
             nc.sync.dma_start(out=te_tile[:], in_=target_embedding[n].rearrange("(p r) e -> p r e", r=Q_TILES))
             te_sb[n] = te_tile
 
-        def sum_squares(ge):
+        def row_scales():
             half = C // 2
-            sumsq_s = work.tile([P, PACK], F32)
-            sumsq_v = work.tile([P, PACK], F32)
-            for t in range(PACK):
-                squares_s = work.tile([P, half], BF16, bufs=1)
-                nc.scalar.activation(
-                    out=squares_s[:], in_=v_sb[ge][:, t, 0:half], func=ACT.Square, accum_out=sumsq_s[:, t : t + 1]
-                )
-                squares_v = work.tile([P, half], F32, bufs=1)
-                nc.vector.scalar_tensor_tensor(
-                    out=squares_v[:],
-                    in0=v_sb[ge][:, t, half:C],
-                    scalar=1.0,
-                    in1=v_sb[ge][:, t, half:C],
-                    op0=ALU.mult,
-                    op1=ALU.mult,
-                    accum_out=sumsq_v[:, t : t + 1],
-                )
-            sumsq[ge] = (sumsq_s, sumsq_v)
-
-        def row_scales(ge):
-            sumsq_s, sumsq_v = sumsq[ge]
-            total = work.tile([P, PACK], F32)
-            nc.vector.tensor_add(out=total[:], in0=sumsq_s[:], in1=sumsq_v[:])
-            norm = work.tile([P, PACK], F32)
-            nc.scalar.activation(out=norm[:], in_=total[:], func=ACT.Sqrt)
-            g_over_norm = work.tile([P, PACK], F32)
+            sumsq_s = const.tile([P, E_TILES], F32)
+            sumsq_v = const.tile([P, E_TILES], F32)
+            for ge in range(E_PASSES):
+                for t in range(PACK):
+                    m = PACK * ge + t
+                    squares_s = work.tile([P, half], BF16, bufs=1)
+                    nc.scalar.activation(
+                        out=squares_s[:], in_=v_sb[ge][:, t, 0:half], func=ACT.Square, accum_out=sumsq_s[:, m : m + 1]
+                    )
+                    squares_v = work.tile([P, half], F32, bufs=1)
+                    nc.vector.scalar_tensor_tensor(
+                        out=squares_v[:],
+                        in0=v_sb[ge][:, t, half:C],
+                        scalar=1.0,
+                        in1=v_sb[ge][:, t, half:C],
+                        op0=ALU.mult,
+                        op1=ALU.mult,
+                        accum_out=sumsq_v[:, m : m + 1],
+                    )
+            sumsq = const.tile([P, E_TILES], F32)
+            nc.vector.tensor_add(out=sumsq[:], in0=sumsq_s[:], in1=sumsq_v[:])
+            norm = const.tile([P, E_TILES], F32)
+            nc.scalar.activation(out=norm[:], in_=sumsq[:], func=ACT.Sqrt)
+            g_over_norm = const.tile([P, E_TILES], F32)
             nc.vector.reciprocal(out=g_over_norm[:], in_=norm[:])
-            nc.vector.tensor_mul(out=g_over_norm[:], in0=g_over_norm[:], in1=gain[:, PACK * ge : PACK * ge + PACK])
-            row_scale[ge] = g_over_norm
+            nc.vector.tensor_mul(out=g_over_norm[:], in0=g_over_norm[:], in1=gain[:])
+            return g_over_norm
 
         def scale_rows(ge):
             for t in range(PACK):
+                m = PACK * ge + t
                 w_tile = work.tile([P, 2 * PACK, P], BF16, bufs=PACK)
                 nc.vector.tensor_scalar(
                     out=w_tile[:].rearrange("p (j w) i -> p j w i", w=2),
                     in0=v_sb[ge][:, t, :].rearrange("p (j i w) -> p j w i", i=P, w=2),
-                    scalar1=row_scale[ge][:, t : t + 1],
+                    scalar1=row_scale[:, m : m + 1],
                     scalar2=None,
                     op0=ALU.mult,
                 )
@@ -128,8 +129,8 @@ def tile_attentionlayer_pa_kernel(
                 in_=w_grouped[ge][:].rearrange("p g e k -> p (g e k)"),
             )
 
-        def transpose_x(n):
-            grouped = work.tile([P, C_PASSES * TQ * PACK], BF16, align_bytes=64, name="x_grouped")
+        def transpose_x(n, copy_on_vector):
+            grouped = work.tile([P, C_PASSES * TQ * PACK], BF16, align_bytes=64, name="x_grouped", bufs=1)
             words = grouped[:].bitcast(F32).rearrange("p (g q u) -> p g q u", g=C_PASSES, u=2)
             for r in range(Q_TILES):
                 x_ps = psum_t.tile([P, 2 * C_PASSES, P], F32, tag="tp")
@@ -137,9 +138,14 @@ def tile_attentionlayer_pa_kernel(
                     nc.tensor.transpose(
                         x_ps[:, j, :], x_sb[n][:, r, :].bitcast(F32)[:, P * j : P * j + P], ident_f32[:]
                     )
-                nc.scalar.copy(
-                    out=words[:, :, P * r : P * r + P, :], in_=x_ps[:].rearrange("p (g u) q -> p g q u", u=2)
-                )
+                if copy_on_vector:
+                    nc.vector.tensor_copy(
+                        out=words[:, :, P * r : P * r + P, :], in_=x_ps[:].rearrange("p (g u) q -> p g q u", u=2)
+                    )
+                else:
+                    nc.scalar.copy(
+                        out=words[:, :, P * r : P * r + P, :], in_=x_ps[:].rearrange("p (g u) q -> p g q u", u=2)
+                    )
             x_grouped[n] = grouped
 
         def quantise_x(n):
@@ -152,26 +158,39 @@ def tile_attentionlayer_pa_kernel(
             )
             x_codes[n], x_scales[n] = codes, scales
 
+        def regrouped_views(grouped, n, ge, sh):
+            chunk = k_sb[n][:, ge, :, N_MOVE * sh : N_MOVE * sh + N_MOVE]
+            return (
+                grouped[:].rearrange("p (c i) t -> p c t i", i=4),
+                chunk.rearrange("p t (c i) -> p c t i", i=4),
+            )
+
+        def regroup_on_scalar(n):
+            ge, sh = SCALAR_CHUNK
+            k_grouped_s = work.tile([P, N_MOVE, PACK], BF16, align_bytes=64)
+            dst, src = regrouped_views(k_grouped_s, n, ge, sh)
+            nc.scalar.copy(out=dst, in_=src)
+            k_from_scalar[n] = k_grouped_s
+
         def quantise_keys(n):
             codes = work.tile([P, E_PASSES, TS], U32, align_bytes=64, name="k_codes")
             scales = work.tile([P, E_PASSES, TS], U8, align_bytes=64, name="k_scales")
             for ge in range(E_PASSES):
-                grouped = []
+                ready = []
+                if ge == SCALAR_CHUNK[0]:
+                    ready.append((SCALAR_CHUNK[1], k_from_scalar[n]))
                 for sh in range(S_HALVES):
-                    k_grouped = work.tile([P, N_MOVE, PACK], BF16, align_bytes=64, bufs=3)
-                    nc.vector.tensor_copy(
-                        out=k_grouped[:].rearrange("p (c i) t -> p c t i", i=4),
-                        in_=k_sb[n][:, ge, :, N_MOVE * sh : N_MOVE * sh + N_MOVE].rearrange(
-                            "p t (c i) -> p c t i", i=4
-                        ),
-                    )
-                    grouped.append(k_grouped)
-                for sh in range(S_HALVES):
+                    if (ge, sh) != SCALAR_CHUNK:
+                        k_grouped = work.tile([P, N_MOVE, PACK], BF16, align_bytes=64, bufs=3)
+                        dst, src = regrouped_views(k_grouped, n, ge, sh)
+                        nc.vector.tensor_copy(out=dst, in_=src)
+                        ready.append((sh, k_grouped))
+                for sh, grouped in ready:
                     s_cols = slice(N_MOVE * sh, N_MOVE * sh + N_MOVE)
                     nc.vector.quantize_mx(
                         out=codes[:, ge, s_cols].bitcast(FP8X4),
                         scales=scales[:, ge, s_cols],
-                        in_=grouped[sh][:].rearrange("p s t -> p (s t)"),
+                        in_=grouped[:].rearrange("p s t -> p (s t)"),
                     )
             k_codes[n], k_scales[n] = codes, scales
 
@@ -197,9 +216,9 @@ def tile_attentionlayer_pa_kernel(
                 h_part[n, ge] = part
 
         def transpose_te(n):
-            for ge in range(E_PASSES):
-                for hq in range(2):
-                    bank = psum_t.tile([P, PACK, 2 * P], BF16, tag="tp", name="te_ps")
+            for hq in range(2):
+                for ge in range(E_PASSES):
+                    bank = psum_t.tile([P, PACK, Q_HALF], BF16, tag="tp", name="te_ps")
                     for t in range(PACK):
                         e0 = K_PASS * ge + P * t
                         for rr in range(2):
@@ -209,33 +228,31 @@ def tile_attentionlayer_pa_kernel(
                     te_ps[n, ge, hq] = bank
 
         def finish_h(n):
-            codes = work.tile([P, E_PASSES, TQ], U32, align_bytes=64, name="h_codes")
-            scales = work.tile([P, E_PASSES, TQ], U8, align_bytes=64, name="h_scales")
-            grouped = []
-            for ge in range(E_PASSES):
-                h_grouped = work.tile([P, TQ, PACK], BF16, align_bytes=64)
-                for hq in range(2):
-                    q_cols = slice(2 * P * hq, 2 * P * hq + 2 * P)
+            codes = work.tile([P, 2, E_PASSES, Q_HALF], U32, align_bytes=64, name="h_codes")
+            scales = work.tile([P, 2, E_PASSES, Q_HALF], U8, align_bytes=64, name="h_scales")
+            for hq in range(2):
+                q_cols = slice(Q_HALF * hq, Q_HALF * hq + Q_HALF)
+                h_grouped = work.tile([P, E_PASSES, Q_HALF, PACK], BF16, align_bytes=64)
+                for ge in range(E_PASSES):
                     nc.vector.scalar_tensor_tensor(
-                        out=h_grouped[:, q_cols, :],
+                        out=h_grouped[:, ge],
                         in0=te_ps[n, ge, hq][:].rearrange("p t q -> p q t"),
                         scalar=SQRT_HALF,
                         in1=h_part[n, ge][:, :, q_cols].rearrange("p t q -> p q t"),
                         op0=ALU.mult,
                         op1=ALU.add,
                     )
-                grouped.append(h_grouped)
-            for ge in range(E_PASSES):
                 nc.vector.quantize_mx(
-                    out=codes[:, ge, :].bitcast(FP8X4),
-                    scales=scales[:, ge, :],
-                    in_=grouped[ge][:].rearrange("p q t -> p (q t)"),
+                    out=codes[:, hq].rearrange("p g q -> p (g q)").bitcast(FP8X4),
+                    scales=scales[:, hq].rearrange("p g q -> p (g q)"),
+                    in_=h_grouped[:].rearrange("p g q t -> p (g q t)"),
                 )
             h_codes[n], h_scales[n] = codes, scales
 
         def scores(n, vector_helps):
             out_rows = out[n].rearrange("(p r) s -> p r s", r=Q_TILES)
             for r in range(Q_TILES):
+                hq, rr = divmod(r, 2)
                 o_sb = work.tile([P, TS], F32, bufs=4)
                 for sh in range(S_HALVES):
                     s_cols = slice(N_MOVE * sh, N_MOVE * sh + N_MOVE)
@@ -243,8 +260,8 @@ def tile_attentionlayer_pa_kernel(
                     for ge in range(E_PASSES):
                         nc.tensor.matmul_mx(
                             out=o_ps[:],
-                            lhsT=h_codes[n][:, ge, P * r : P * r + P].bitcast(FP8X4),
-                            lhsT_scale=h_scales[n][:, ge, P * r : P * r + P],
+                            lhsT=h_codes[n][:, hq, ge, P * rr : P * rr + P].bitcast(FP8X4),
+                            lhsT_scale=h_scales[n][:, hq, ge, P * rr : P * rr + P],
                             rhs=k_codes[n][:, ge, s_cols].bitcast(FP8X4),
                             rhs_scale=k_scales[n][:, ge, s_cols],
                             start=(ge == 0),
@@ -287,23 +304,22 @@ def tile_attentionlayer_pa_kernel(
         w_codes = const.tile([P, E_PASSES, C_PASSES, K_PASS], U32, align_bytes=64)
         w_scales = const.tile([P, E_PASSES, C_PASSES, K_PASS], U8, align_bytes=64)
 
-        sum_squares(0)
-        row_scales(0)
+        row_scale = row_scales()
         scale_rows(0)
-        sum_squares(1)
-        transpose_w(0)
-        row_scales(1)
-        quantise_w(0)
         scale_rows(1)
-        transpose_x(0)
+        transpose_w(0)
+        transpose_x(0, copy_on_vector=True)
         transpose_w(1)
+        quantise_w(0)
         quantise_x(0)
+        transpose_x(1, copy_on_vector=False)
+        regroup_on_scalar(0)
         quantise_w(1)
         project(0)
-        transpose_x(1)
         transpose_te(0)
         quantise_keys(0)
         quantise_x(1)
+        regroup_on_scalar(1)
 
         for n in range(BATCH):
             if n + 2 < BATCH:
@@ -314,10 +330,11 @@ def tile_attentionlayer_pa_kernel(
             if n + 1 < BATCH:
                 project(n + 1)
             if n + 2 < BATCH:
-                transpose_x(n + 2)
+                transpose_x(n + 2, copy_on_vector=False)
             if n + 1 < BATCH:
                 transpose_te(n + 1)
                 quantise_keys(n + 1)
             if n + 2 < BATCH:
                 quantise_x(n + 2)
+                regroup_on_scalar(n + 2)
         scores(BATCH - 1, vector_helps=True)

@@ -91,6 +91,10 @@ def tile_attentionlayer_pa_kernel(
                     )
             sumsq = const.tile([P, E_TILES], F32)
             nc.vector.tensor_add(out=sumsq[:], in0=sumsq_s[:], in1=sumsq_v[:])
+            nc.vector.tensor_copy(out=gain[:], in_=gb_ps[:, 0:E_TILES])
+            nc.vector.tensor_scalar(
+                out=bias_s[:], in0=gb_ps[:, E_TILES : 2 * E_TILES], scalar1=SQRT_HALF, scalar2=None, op0=ALU.mult
+            )
             norm = const.tile([P, E_TILES], F32)
             nc.scalar.activation(out=norm[:], in_=sumsq[:], func=ACT.Sqrt)
             g_over_norm = const.tile([P, E_TILES], F32)
@@ -101,22 +105,19 @@ def tile_attentionlayer_pa_kernel(
         def scale_rows(ge):
             for t in range(PACK):
                 m = PACK * ge + t
-                w_tile = work.tile([P, 2 * PACK, P], BF16, bufs=PACK)
+                w_tile = work.tile([P, C], BF16, bufs=PACK)
                 nc.vector.tensor_scalar(
-                    out=w_tile[:].rearrange("p (j w) i -> p j w i", w=2),
-                    in0=v_sb[ge][:, t, :].rearrange("p (j i w) -> p j w i", i=P, w=2),
-                    scalar1=row_scale[:, m : m + 1],
-                    scalar2=None,
-                    op0=ALU.mult,
+                    out=w_tile[:], in0=v_sb[ge][:, t, :], scalar1=row_scale[:, m : m + 1], scalar2=None, op0=ALU.mult
                 )
                 w_rows[ge, t] = w_tile
 
         def transpose_w(ge):
             grouped = work.tile([P, C_PASSES, K_PASS, PACK], BF16, align_bytes=64, name="w_grouped")
             for t in range(PACK):
+                blocks = w_rows[ge, t][:].rearrange("p (j i w) -> p j w i", i=P, w=2)
                 w_ps = psum_t.tile([P, 2 * PACK, P], BF16, tag="tp")
                 for blk in range(2 * PACK):
-                    nc.tensor.transpose(w_ps[:, blk, :], w_rows[ge, t][:, blk, :], ident_bf[:])
+                    nc.tensor.transpose(w_ps[:, blk, :], blocks[:, blk // 2, blk % 2, :], ident_bf[:])
                 nc.scalar.copy(
                     out=grouped[:, :, P * t : P * t + P, :], in_=w_ps[:].rearrange("p (g k) e -> p g e k", k=PACK)
                 )
@@ -230,23 +231,35 @@ def tile_attentionlayer_pa_kernel(
         def finish_h(n):
             codes = work.tile([P, 2, E_PASSES, Q_HALF], U32, align_bytes=64, name="h_codes")
             scales = work.tile([P, 2, E_PASSES, Q_HALF], U8, align_bytes=64, name="h_scales")
+            grouped = {}
             for hq in range(2):
-                q_cols = slice(Q_HALF * hq, Q_HALF * hq + Q_HALF)
                 h_grouped = work.tile([P, E_PASSES, Q_HALF, PACK], BF16, align_bytes=64)
-                for ge in range(E_PASSES):
-                    nc.vector.scalar_tensor_tensor(
-                        out=h_grouped[:, ge],
-                        in0=te_ps[n, ge, hq][:].rearrange("p t q -> p q t"),
-                        scalar=SQRT_HALF,
-                        in1=h_part[n, ge][:, :, q_cols].rearrange("p t q -> p q t"),
-                        op0=ALU.mult,
-                        op1=ALU.add,
-                    )
+                grouped[hq] = h_grouped
+
+            def add_embedding(hq, ge):
+                q_cols = slice(Q_HALF * hq, Q_HALF * hq + Q_HALF)
+                nc.vector.scalar_tensor_tensor(
+                    out=grouped[hq][:, ge],
+                    in0=te_ps[n, ge, hq][:].rearrange("p t q -> p q t"),
+                    scalar=SQRT_HALF,
+                    in1=h_part[n, ge][:, :, q_cols].rearrange("p t q -> p q t"),
+                    op0=ALU.mult,
+                    op1=ALU.add,
+                )
+
+            def quantise_half(hq):
                 nc.vector.quantize_mx(
                     out=codes[:, hq].rearrange("p g q -> p (g q)").bitcast(FP8X4),
                     scales=scales[:, hq].rearrange("p g q -> p (g q)"),
-                    in_=h_grouped[:].rearrange("p g q t -> p (g q t)"),
+                    in_=grouped[hq][:].rearrange("p g q t -> p (g q t)"),
                 )
+
+            add_embedding(0, 0)
+            add_embedding(0, 1)
+            add_embedding(1, 0)
+            quantise_half(0)
+            add_embedding(1, 1)
+            quantise_half(1)
             h_codes[n], h_scales[n] = codes, scales
 
         def scores(n, vector_helps):
@@ -278,6 +291,11 @@ def tile_attentionlayer_pa_kernel(
         load_batch(0)
         load_batch(1)
 
+        gb_rows = const.tile([P, P], BF16)
+        nc.vector.memset(gb_rows[:], 0.0)
+        nc.scalar.dma_start(out=gb_rows[0:E_TILES, :], in_=in_proj_g.rearrange("(m p) -> m p", p=P))
+        nc.scalar.dma_start(out=gb_rows[E_TILES : 2 * E_TILES, :], in_=in_proj_b.rearrange("(m p) -> m p", p=P))
+
         one = const.tile([P, 1], F32)
         nc.vector.memset(one[:], 1.0)
         warm = const.tile([P, 1], F32)
@@ -288,18 +306,10 @@ def tile_attentionlayer_pa_kernel(
         ident_f32 = const.tile([P, P], F32)
         make_identity(nc, ident_f32[:])
 
-        gb_rows = const.tile([P, P], BF16)
-        nc.vector.memset(gb_rows[:], 0.0)
-        nc.scalar.dma_start(out=gb_rows[0:E_TILES, :], in_=in_proj_g.rearrange("(m p) -> m p", p=P))
-        nc.scalar.dma_start(out=gb_rows[E_TILES : 2 * E_TILES, :], in_=in_proj_b.rearrange("(m p) -> m p", p=P))
         gb_ps = psum_t.tile([P, P], BF16, tag="tp")
         nc.tensor.transpose(gb_ps[:], gb_rows[:], ident_bf[:])
         gain = const.tile([P, E_TILES], F32)
-        nc.vector.tensor_copy(out=gain[:], in_=gb_ps[:, 0:E_TILES])
         bias_s = const.tile([P, E_TILES], F32)
-        nc.vector.tensor_scalar(
-            out=bias_s[:], in0=gb_ps[:, E_TILES : 2 * E_TILES], scalar1=SQRT_HALF, scalar2=None, op0=ALU.mult
-        )
 
         w_codes = const.tile([P, E_PASSES, C_PASSES, K_PASS], U32, align_bytes=64)
         w_scales = const.tile([P, E_PASSES, C_PASSES, K_PASS], U8, align_bytes=64)

@@ -284,7 +284,7 @@ def tile_attentionlayer_pa_kernel(
                         nc.vector.tensor_copy(out=o_sb[:, s_cols], in_=o_ps[:])
                     else:
                         nc.scalar.copy(out=o_sb[:, s_cols], in_=o_ps[:])
-                nc.sync.dma_start(out=out_rows[:, r, :], in_=o_sb[:])
+                    nc.sync.dma_start(out=out_rows[:, r, s_cols], in_=o_sb[:, s_cols])
 
         for ge in range(E_PASSES):
             load_v(ge)
@@ -337,11 +337,10 @@ def tile_attentionlayer_pa_kernel(
             finish_h(n)
             if n >= 1:
                 scores(n - 1, vector_helps=False)
-            if n + 1 < BATCH:
-                project(n + 1)
             if n + 2 < BATCH:
                 transpose_x(n + 2, copy_on_vector=False)
             if n + 1 < BATCH:
+                project(n + 1)
                 transpose_te(n + 1)
                 quantise_keys(n + 1)
             if n + 2 < BATCH:

@@ -55,71 +55,78 @@ def tile_attentionlayer_pa_kernel(
                 nc.sync.dma_start(out=v_tile[:, t, :], in_=in_proj_v[row0 : row0 + P, :])
             v_sb[ge] = v_tile
 
-        def load_batch(n):
+        def load_x(n):
             x_tile = raw.tile([P, Q_TILES, C], BF16)
             nc.sync.dma_start(out=x_tile[:], in_=x[n].rearrange("(p r) c -> p r c", r=Q_TILES))
             x_sb[n] = x_tile
+
+        def load_keys(n):
             k_tile = raw.tile([P, E_PASSES, PACK, TS], BF16)
             for ge in range(E_PASSES):
                 rows = encoder_keys[n][K_PASS * ge : K_PASS * ge + K_PASS, :]
                 nc.sync.dma_start(out=k_tile[:, ge], in_=rows.rearrange("(t p) s -> p t s", p=P))
             k_sb[n] = k_tile
+
+        def load_te(n):
             te_tile = raw.tile([P, Q_TILES, E], BF16)
             nc.sync.dma_start(out=te_tile[:], in_=target_embedding[n].rearrange("(p r) e -> p r e", r=Q_TILES))
             te_sb[n] = te_tile
 
-        def row_scales():
-            half = C // 2
-            sumsq_s = const.tile([P, E_TILES], F32)
-            sumsq_v = const.tile([P, E_TILES], F32)
-            for ge in range(E_PASSES):
-                for t in range(PACK):
-                    m = PACK * ge + t
-                    squares_s = work.tile([P, half], BF16, bufs=1)
-                    nc.scalar.activation(
-                        out=squares_s[:], in_=v_sb[ge][:, t, 0:half], func=ACT.Square, accum_out=sumsq_s[:, m : m + 1]
-                    )
-                    squares_v = work.tile([P, half], F32, bufs=1)
-                    nc.vector.scalar_tensor_tensor(
-                        out=squares_v[:],
-                        in0=v_sb[ge][:, t, half:C],
-                        scalar=1.0,
-                        in1=v_sb[ge][:, t, half:C],
-                        op0=ALU.mult,
-                        op1=ALU.mult,
-                        accum_out=sumsq_v[:, m : m + 1],
-                    )
-            sumsq = const.tile([P, E_TILES], F32)
-            nc.vector.tensor_add(out=sumsq[:], in0=sumsq_s[:], in1=sumsq_v[:])
-            nc.vector.tensor_copy(out=gain[:], in_=gb_ps[:, 0:E_TILES])
-            nc.vector.tensor_scalar(
-                out=bias_s[:], in0=gb_ps[:, E_TILES : 2 * E_TILES], scalar1=SQRT_HALF, scalar2=None, op0=ALU.mult
-            )
-            norm = const.tile([P, E_TILES], F32)
-            nc.scalar.activation(out=norm[:], in_=sumsq[:], func=ACT.Sqrt)
-            g_over_norm = const.tile([P, E_TILES], F32)
-            nc.vector.reciprocal(out=g_over_norm[:], in_=norm[:])
-            nc.vector.tensor_mul(out=g_over_norm[:], in0=g_over_norm[:], in1=gain[:])
-            return g_over_norm
+        def load_batch(n):
+            load_x(n)
+            load_keys(n)
+            load_te(n)
 
-        def scale_rows(ge):
-            for t in range(PACK):
-                m = PACK * ge + t
-                w_tile = work.tile([P, C], BF16, bufs=PACK)
-                nc.vector.tensor_scalar(
-                    out=w_tile[:], in0=v_sb[ge][:, t, :], scalar1=row_scale[:, m : m + 1], scalar2=None, op0=ALU.mult
-                )
-                w_rows[ge, t] = w_tile
+        def sum_squares(ge, t):
+            half = C // 2
+            m = PACK * ge + t
+            squares_s = work.tile([P, half], BF16, bufs=1)
+            nc.scalar.activation(
+                out=squares_s[:], in_=v_sb[ge][:, t, 0:half], func=ACT.Square, accum_out=sumsq_s[:, m : m + 1]
+            )
+            squares_v = work.tile([P, half], F32, bufs=1)
+            nc.vector.scalar_tensor_tensor(
+                out=squares_v[:],
+                in0=v_sb[ge][:, t, half:C],
+                scalar=1.0,
+                in1=v_sb[ge][:, t, half:C],
+                op0=ALU.mult,
+                op1=ALU.mult,
+                accum_out=sumsq_v[:, m : m + 1],
+            )
+
+        def norm_columns(ge):
+            cols = slice(PACK * ge, PACK * ge + PACK)
+            nc.vector.tensor_add(out=sumsq[:, cols], in0=sumsq_s[:, cols], in1=sumsq_v[:, cols])
+            nc.scalar.activation(out=norm[:, cols], in_=sumsq[:, cols], func=ACT.Sqrt)
+
+        def invert_norm(ge):
+            cols = slice(PACK * ge, PACK * ge + PACK)
+            nc.vector.reciprocal(out=inv_norm[:, cols], in_=norm[:, cols])
+
+        def times_gain(ge):
+            cols = slice(PACK * ge, PACK * ge + PACK)
+            nc.vector.tensor_mul(out=row_scale[:, cols], in0=inv_norm[:, cols], in1=gain[:, cols])
+
+        def scale_rows(ge, t):
+            m = PACK * ge + t
+            w_tile = work.tile([P, C], BF16, bufs=2 * PACK)
+            nc.vector.tensor_scalar(
+                out=w_tile[:], in0=v_sb[ge][:, t, :], scalar1=row_scale[:, m : m + 1], scalar2=None, op0=ALU.mult
+            )
+            w_rows[ge, t] = w_tile
 
         def transpose_w(ge):
-            grouped = work.tile([P, C_PASSES, K_PASS, PACK], BF16, align_bytes=64, name="w_grouped")
+            grouped = work.tile([P, C_PASSES * K_PASS * PACK], BF16, align_bytes=64, name="w_grouped")
+            words = grouped[:].bitcast(F32).rearrange("p (g e u) -> p g e u", g=C_PASSES, u=2)
             for t in range(PACK):
-                blocks = w_rows[ge, t][:].rearrange("p (j i w) -> p j w i", i=P, w=2)
-                w_ps = psum_t.tile([P, 2 * PACK, P], BF16, tag="tp")
-                for blk in range(2 * PACK):
-                    nc.tensor.transpose(w_ps[:, blk, :], blocks[:, blk // 2, blk % 2, :], ident_bf[:])
+                w_ps = psum_t.tile([P, 2 * C_PASSES, P], F32, tag="tp")
+                for j in range(2 * C_PASSES):
+                    nc.tensor.transpose(
+                        w_ps[:, j, :], w_rows[ge, t][:].bitcast(F32)[:, P * j : P * j + P], ident_f32[:]
+                    )
                 nc.scalar.copy(
-                    out=grouped[:, :, P * t : P * t + P, :], in_=w_ps[:].rearrange("p (g k) e -> p g e k", k=PACK)
+                    out=words[:, :, P * t : P * t + P, :], in_=w_ps[:].rearrange("p (g u) e -> p g e u", u=2)
                 )
             w_grouped[ge] = grouped
 
@@ -127,14 +134,14 @@ def tile_attentionlayer_pa_kernel(
             nc.vector.quantize_mx(
                 out=w_codes[:, ge].rearrange("p g e -> p (g e)").bitcast(FP8X4),
                 scales=w_scales[:, ge].rearrange("p g e -> p (g e)"),
-                in_=w_grouped[ge][:].rearrange("p g e k -> p (g e k)"),
+                in_=w_grouped[ge][:],
             )
 
-        def transpose_x(n, copy_on_vector):
+        def transpose_x(n, copy_on_vector, pool, tag):
             grouped = work.tile([P, C_PASSES * TQ * PACK], BF16, align_bytes=64, name="x_grouped", bufs=1)
             words = grouped[:].bitcast(F32).rearrange("p (g q u) -> p g q u", g=C_PASSES, u=2)
             for r in range(Q_TILES):
-                x_ps = psum_t.tile([P, 2 * C_PASSES, P], F32, tag="tp")
+                x_ps = pool.tile([P, 2 * C_PASSES, P], F32, tag=tag)
                 for j in range(2 * C_PASSES):
                     nc.tensor.transpose(
                         x_ps[:, j, :], x_sb[n][:, r, :].bitcast(F32)[:, P * j : P * j + P], ident_f32[:]
@@ -288,8 +295,12 @@ def tile_attentionlayer_pa_kernel(
 
         for ge in range(E_PASSES):
             load_v(ge)
-        load_batch(0)
-        load_batch(1)
+        load_x(0)
+        load_keys(0)
+        load_x(1)
+        load_te(0)
+        load_keys(1)
+        load_te(1)
 
         gb_rows = const.tile([P, P], BF16)
         nc.vector.memset(gb_rows[:], 0.0)
@@ -314,15 +325,41 @@ def tile_attentionlayer_pa_kernel(
         w_codes = const.tile([P, E_PASSES, C_PASSES, K_PASS], U32, align_bytes=64)
         w_scales = const.tile([P, E_PASSES, C_PASSES, K_PASS], U8, align_bytes=64)
 
-        row_scale = row_scales()
-        scale_rows(0)
-        scale_rows(1)
+        sumsq_s = const.tile([P, E_TILES], F32)
+        sumsq_v = const.tile([P, E_TILES], F32)
+        sumsq = const.tile([P, E_TILES], F32)
+        norm = const.tile([P, E_TILES], F32)
+        inv_norm = const.tile([P, E_TILES], F32)
+        row_scale = const.tile([P, E_TILES], F32)
+
+        for t in range(PACK):
+            sum_squares(0, t)
+        sum_squares(1, 0)
+        sum_squares(1, 1)
+        norm_columns(0)
+        nc.vector.tensor_copy(out=gain[:], in_=gb_ps[:, 0:E_TILES])
+        nc.vector.tensor_scalar(
+            out=bias_s[:], in0=gb_ps[:, E_TILES : 2 * E_TILES], scalar1=SQRT_HALF, scalar2=None, op0=ALU.mult
+        )
+        sum_squares(1, 2)
+        invert_norm(0)
+        sum_squares(1, 3)
+        times_gain(0)
+        norm_columns(1)
+        scale_rows(0, 0)
+        scale_rows(0, 1)
+        invert_norm(1)
+        scale_rows(0, 2)
+        times_gain(1)
+        scale_rows(0, 3)
+        for t in range(PACK):
+            scale_rows(1, t)
         transpose_w(0)
-        transpose_x(0, copy_on_vector=True)
+        transpose_x(0, copy_on_vector=True, pool=psum_mx, tag="mx")
         transpose_w(1)
         quantise_w(0)
         quantise_x(0)
-        transpose_x(1, copy_on_vector=False)
+        transpose_x(1, copy_on_vector=False, pool=psum_t, tag="tp")
         regroup_on_scalar(0)
         quantise_w(1)
         project(0)
@@ -338,7 +375,7 @@ def tile_attentionlayer_pa_kernel(
             if n >= 1:
                 scores(n - 1, vector_helps=False)
             if n + 2 < BATCH:
-                transpose_x(n + 2, copy_on_vector=False)
+                transpose_x(n + 2, copy_on_vector=False, pool=psum_t, tag="tp")
             if n + 1 < BATCH:
                 project(n + 1)
                 transpose_te(n + 1)

@@ -26,6 +26,7 @@ Q_HALF = TQ // 2
 S_HALVES = TS // N_MOVE
 SQRT_HALF = math.sqrt(0.5)
 SCALAR_CHUNK = (1, 1)
+GPSIMD_CHUNK = (1, 0)
 
 FLOPS = 2 * BATCH * TQ * C * E + 2 * BATCH * TQ * E * TS
 
@@ -37,7 +38,7 @@ def tile_attentionlayer_pa_kernel(
     with ExitStack() as stack:
         stack.enter_context(tc.manual_schedule())
         const = stack.enter_context(tc.tile_pool(name="const", bufs=1))
-        raw = stack.enter_context(tc.tile_pool(name="raw", bufs=2))
+        raw = stack.enter_context(tc.tile_pool(name="raw", bufs=10))
         work = stack.enter_context(tc.tile_pool(name="work", bufs=2))
         psum_t = stack.enter_context(tc.psum_pool(name="psum_t", bufs=4))
         psum_mx = stack.enter_context(tc.psum_pool(name="psum_mx", bufs=4))
@@ -45,30 +46,30 @@ def tile_attentionlayer_pa_kernel(
         v_sb, w_rows, w_grouped = {}, {}, {}
         x_sb, k_sb, te_sb = {}, {}, {}
         x_grouped, x_codes, x_scales = {}, {}, {}
-        k_from_scalar, k_codes, k_scales = {}, {}, {}
+        k_from_scalar, k_from_gpsimd, k_codes, k_scales = {}, {}, {}, {}
         h_part, te_ps, h_codes, h_scales = {}, {}, {}, {}
 
         def load_v(ge):
-            v_tile = raw.tile([P, PACK, C], BF16)
+            v_tile = raw.tile([P, PACK, C], BF16, tag="raw")
             for t in range(PACK):
                 row0 = K_PASS * ge + P * t
                 nc.sync.dma_start(out=v_tile[:, t, :], in_=in_proj_v[row0 : row0 + P, :])
             v_sb[ge] = v_tile
 
         def load_x(n):
-            x_tile = raw.tile([P, Q_TILES, C], BF16)
+            x_tile = raw.tile([P, Q_TILES, C], BF16, tag="raw")
             nc.sync.dma_start(out=x_tile[:], in_=x[n].rearrange("(p r) c -> p r c", r=Q_TILES))
             x_sb[n] = x_tile
 
         def load_keys(n):
-            k_tile = raw.tile([P, E_PASSES, PACK, TS], BF16)
             for ge in range(E_PASSES):
+                k_tile = raw.tile([P, PACK, TS], BF16, tag="raw")
                 rows = encoder_keys[n][K_PASS * ge : K_PASS * ge + K_PASS, :]
-                nc.sync.dma_start(out=k_tile[:, ge], in_=rows.rearrange("(t p) s -> p t s", p=P))
-            k_sb[n] = k_tile
+                nc.sync.dma_start(out=k_tile[:], in_=rows.rearrange("(t p) s -> p t s", p=P))
+                k_sb[n, ge] = k_tile
 
         def load_te(n):
-            te_tile = raw.tile([P, Q_TILES, E], BF16)
+            te_tile = raw.tile([P, Q_TILES, E], BF16, tag="raw")
             nc.sync.dma_start(out=te_tile[:], in_=target_embedding[n].rearrange("(p r) e -> p r e", r=Q_TILES))
             te_sb[n] = te_tile
 
@@ -125,9 +126,12 @@ def tile_attentionlayer_pa_kernel(
                     nc.tensor.transpose(
                         w_ps[:, j, :], w_rows[ge, t][:].bitcast(F32)[:, P * j : P * j + P], ident_f32[:]
                     )
-                nc.scalar.copy(
-                    out=words[:, :, P * t : P * t + P, :], in_=w_ps[:].rearrange("p (g u) e -> p g e u", u=2)
-                )
+                dst = words[:, :, P * t : P * t + P, :]
+                src = w_ps[:].rearrange("p (g u) e -> p g e u", u=2)
+                if t % 2 == 0:
+                    nc.vector.tensor_copy(out=dst, in_=src)
+                else:
+                    nc.scalar.copy(out=dst, in_=src)
             w_grouped[ge] = grouped
 
         def quantise_w(ge):
@@ -137,7 +141,7 @@ def tile_attentionlayer_pa_kernel(
                 in_=w_grouped[ge][:],
             )
 
-        def transpose_x(n, copy_on_vector, pool, tag):
+        def transpose_x(n, pool, tag):
             grouped = work.tile([P, C_PASSES * TQ * PACK], BF16, align_bytes=64, name="x_grouped", bufs=1)
             words = grouped[:].bitcast(F32).rearrange("p (g q u) -> p g q u", g=C_PASSES, u=2)
             for r in range(Q_TILES):
@@ -146,14 +150,9 @@ def tile_attentionlayer_pa_kernel(
                     nc.tensor.transpose(
                         x_ps[:, j, :], x_sb[n][:, r, :].bitcast(F32)[:, P * j : P * j + P], ident_f32[:]
                     )
-                if copy_on_vector:
-                    nc.vector.tensor_copy(
-                        out=words[:, :, P * r : P * r + P, :], in_=x_ps[:].rearrange("p (g u) q -> p g q u", u=2)
-                    )
-                else:
-                    nc.scalar.copy(
-                        out=words[:, :, P * r : P * r + P, :], in_=x_ps[:].rearrange("p (g u) q -> p g q u", u=2)
-                    )
+                nc.scalar.copy(
+                    out=words[:, :, P * r : P * r + P, :], in_=x_ps[:].rearrange("p (g u) q -> p g q u", u=2)
+                )
             x_grouped[n] = grouped
 
         def quantise_x(n):
@@ -167,7 +166,7 @@ def tile_attentionlayer_pa_kernel(
             x_codes[n], x_scales[n] = codes, scales
 
         def regrouped_views(grouped, n, ge, sh):
-            chunk = k_sb[n][:, ge, :, N_MOVE * sh : N_MOVE * sh + N_MOVE]
+            chunk = k_sb[n, ge][:, :, N_MOVE * sh : N_MOVE * sh + N_MOVE]
             return (
                 grouped[:].rearrange("p (c i) t -> p c t i", i=4),
                 chunk.rearrange("p t (c i) -> p c t i", i=4),
@@ -180,27 +179,47 @@ def tile_attentionlayer_pa_kernel(
             nc.scalar.copy(out=dst, in_=src)
             k_from_scalar[n] = k_grouped_s
 
-        def quantise_keys(n):
+        def regroup_on_vector(n, ge, sh):
+            k_grouped = work.tile([P, N_MOVE, PACK], BF16, align_bytes=64, bufs=3)
+            dst, src = regrouped_views(k_grouped, n, ge, sh)
+            nc.vector.tensor_copy(out=dst, in_=src)
+            return k_grouped
+
+        def regroup_on_gpsimd(n):
+            ge, sh = GPSIMD_CHUNK
+            go = work.tile([P, 1], F32)
+            nc.vector.memset(go[:], 1.0)
+            k_grouped_g = work.tile([P, N_MOVE, PACK], BF16, align_bytes=64, bufs=1)
+            nc.gpsimd.tensor_scalar(
+                out=k_grouped_g[:],
+                in0=k_sb[n, ge][:, :, N_MOVE * sh : N_MOVE * sh + N_MOVE].rearrange("p t c -> p c t"),
+                scalar1=go[:],
+                scalar2=0.0,
+                op0=ALU.mult,
+                op1=ALU.add,
+            )
+            k_from_gpsimd[n] = k_grouped_g
+
+        def quantise_chunk(n, ge, sh, grouped):
+            s_cols = slice(N_MOVE * sh, N_MOVE * sh + N_MOVE)
+            nc.vector.quantize_mx(
+                out=k_codes[n][:, ge, s_cols].bitcast(FP8X4),
+                scales=k_scales[n][:, ge, s_cols],
+                in_=grouped[:].rearrange("p s t -> p (s t)"),
+            )
+
+        def quantise_keys(n, x_batch):
             codes = work.tile([P, E_PASSES, TS], U32, align_bytes=64, name="k_codes")
             scales = work.tile([P, E_PASSES, TS], U8, align_bytes=64, name="k_scales")
-            for ge in range(E_PASSES):
-                ready = []
-                if ge == SCALAR_CHUNK[0]:
-                    ready.append((SCALAR_CHUNK[1], k_from_scalar[n]))
-                for sh in range(S_HALVES):
-                    if (ge, sh) != SCALAR_CHUNK:
-                        k_grouped = work.tile([P, N_MOVE, PACK], BF16, align_bytes=64, bufs=3)
-                        dst, src = regrouped_views(k_grouped, n, ge, sh)
-                        nc.vector.tensor_copy(out=dst, in_=src)
-                        ready.append((sh, k_grouped))
-                for sh, grouped in ready:
-                    s_cols = slice(N_MOVE * sh, N_MOVE * sh + N_MOVE)
-                    nc.vector.quantize_mx(
-                        out=codes[:, ge, s_cols].bitcast(FP8X4),
-                        scales=scales[:, ge, s_cols],
-                        in_=grouped[:].rearrange("p s t -> p (s t)"),
-                    )
             k_codes[n], k_scales[n] = codes, scales
+            chunk_00 = regroup_on_vector(n, 0, 0)
+            chunk_01 = regroup_on_vector(n, 0, 1)
+            quantise_chunk(n, 0, 0, chunk_00)
+            chunk_10 = k_from_gpsimd[n] if n in k_from_gpsimd else regroup_on_vector(n, 1, 0)
+            quantise_chunk(n, 0, 1, chunk_01)
+            if x_batch < BATCH:
+                quantise_x(x_batch)
+            quantise_chunk(n, 1, 0, chunk_10)
 
         def project(n):
             for ge in range(E_PASSES):
@@ -235,7 +254,7 @@ def tile_attentionlayer_pa_kernel(
                             )
                     te_ps[n, ge, hq] = bank
 
-        def finish_h(n):
+        def finish_h(n, x_batch=BATCH):
             codes = work.tile([P, 2, E_PASSES, Q_HALF], U32, align_bytes=64, name="h_codes")
             scales = work.tile([P, 2, E_PASSES, Q_HALF], U8, align_bytes=64, name="h_scales")
             grouped = {}
@@ -261,11 +280,12 @@ def tile_attentionlayer_pa_kernel(
                     in_=grouped[hq][:].rearrange("p g q t -> p (g q t)"),
                 )
 
-            add_embedding(0, 0)
-            add_embedding(0, 1)
-            add_embedding(1, 0)
+            for hq in range(2):
+                for ge in range(E_PASSES):
+                    add_embedding(hq, ge)
+            if x_batch < BATCH:
+                quantise_x(x_batch)
             quantise_half(0)
-            add_embedding(1, 1)
             quantise_half(1)
             h_codes[n], h_scales[n] = codes, scales
 
@@ -295,12 +315,8 @@ def tile_attentionlayer_pa_kernel(
 
         for ge in range(E_PASSES):
             load_v(ge)
-        load_x(0)
-        load_keys(0)
-        load_x(1)
-        load_te(0)
-        load_keys(1)
-        load_te(1)
+        load_batch(0)
+        load_batch(1)
 
         gb_rows = const.tile([P, P], BF16)
         nc.vector.memset(gb_rows[:], 0.0)
@@ -354,33 +370,36 @@ def tile_attentionlayer_pa_kernel(
         scale_rows(0, 3)
         for t in range(PACK):
             scale_rows(1, t)
+        transpose_x(0, pool=psum_mx, tag="mx")
         transpose_w(0)
-        transpose_x(0, copy_on_vector=True, pool=psum_mx, tag="mx")
-        transpose_w(1)
-        quantise_w(0)
         quantise_x(0)
-        transpose_x(1, copy_on_vector=False, pool=psum_t, tag="tp")
-        regroup_on_scalar(0)
+        quantise_w(0)
+        transpose_w(1)
         quantise_w(1)
         project(0)
         transpose_te(0)
-        quantise_keys(0)
-        quantise_x(1)
+        transpose_x(1, pool=psum_mx, tag="mx")
+        regroup_on_scalar(0)
         regroup_on_scalar(1)
+        quantise_keys(0, x_batch=BATCH)
 
         for n in range(BATCH):
             if n + 2 < BATCH:
                 load_batch(n + 2)
-            finish_h(n)
+            if n + 1 < BATCH:
+                regroup_on_gpsimd(n + 1)
+            finish_h(n, x_batch=1 if n == 0 else BATCH)
+            if n == 0:
+                quantise_chunk(0, *SCALAR_CHUNK, k_from_scalar[0])
             if n >= 1:
                 scores(n - 1, vector_helps=False)
             if n + 2 < BATCH:
-                transpose_x(n + 2, copy_on_vector=False, pool=psum_t, tag="tp")
+                transpose_x(n + 2, pool=psum_t, tag="tp")
             if n + 1 < BATCH:
                 project(n + 1)
                 transpose_te(n + 1)
-                quantise_keys(n + 1)
+                quantise_keys(n + 1, x_batch=n + 2)
+                quantise_chunk(n + 1, *SCALAR_CHUNK, k_from_scalar[n + 1])
             if n + 2 < BATCH:
-                quantise_x(n + 2)
                 regroup_on_scalar(n + 2)
         scores(BATCH - 1, vector_helps=True)

@@ -25,8 +25,7 @@ Q_TILES = TQ // P
 Q_HALF = TQ // 2
 S_HALVES = TS // N_MOVE
 SQRT_HALF = math.sqrt(0.5)
-SCALAR_CHUNK = (1, 1)
-GPSIMD_CHUNK = (1, 0)
+SCALAR_FROM = 768
 
 FLOPS = 2 * BATCH * TQ * C * E + 2 * BATCH * TQ * E * TS
 
@@ -46,8 +45,8 @@ def tile_attentionlayer_pa_kernel(
         v_sb, w_rows, w_grouped = {}, {}, {}
         x_sb, k_sb, te_sb = {}, {}, {}
         x_grouped, x_codes, x_scales = {}, {}, {}
-        k_from_scalar, k_from_gpsimd, k_codes, k_scales = {}, {}, {}, {}
-        h_part, te_ps, h_codes, h_scales = {}, {}, {}, {}
+        k_grouped, k_codes, k_scales = {}, {}, {}
+        h_part, te_ps, h_codes, h_scales, h_cols = {}, {}, {}, {}, {}
 
         def load_v(ge):
             v_tile = raw.tile([P, PACK, C], BF16, tag="raw")
@@ -72,11 +71,6 @@ def tile_attentionlayer_pa_kernel(
             te_tile = raw.tile([P, Q_TILES, E], BF16, tag="raw")
             nc.sync.dma_start(out=te_tile[:], in_=target_embedding[n].rearrange("(p r) e -> p r e", r=Q_TILES))
             te_sb[n] = te_tile
-
-        def load_batch(n):
-            load_x(n)
-            load_keys(n)
-            load_te(n)
 
         def sum_squares(ge, t):
             half = C // 2
@@ -109,22 +103,24 @@ def tile_attentionlayer_pa_kernel(
             cols = slice(PACK * ge, PACK * ge + PACK)
             nc.vector.tensor_mul(out=row_scale[:, cols], in0=inv_norm[:, cols], in1=gain[:, cols])
 
+        def new_w_rows(ge):
+            rows = work.tile([P, PACK, C], BF16, tag="rows_or_part", bufs=4)
+            w_rows[ge] = rows
+
         def scale_rows(ge, t):
             m = PACK * ge + t
-            w_tile = work.tile([P, C], BF16, bufs=2 * PACK)
             nc.vector.tensor_scalar(
-                out=w_tile[:], in0=v_sb[ge][:, t, :], scalar1=row_scale[:, m : m + 1], scalar2=None, op0=ALU.mult
+                out=w_rows[ge][:, t, :], in0=v_sb[ge][:, t, :], scalar1=row_scale[:, m : m + 1], scalar2=None, op0=ALU.mult
             )
-            w_rows[ge, t] = w_tile
 
-        def transpose_w(ge):
-            grouped = work.tile([P, C_PASSES * K_PASS * PACK], BF16, align_bytes=64, name="w_grouped")
+        def transpose_w(ge, pool, tag):
+            grouped = work.tile([P, C_PASSES * K_PASS * PACK], BF16, align_bytes=64, tag="grouped", bufs=3, name="w_grouped")
             words = grouped[:].bitcast(F32).rearrange("p (g e u) -> p g e u", g=C_PASSES, u=2)
             for t in range(PACK):
-                w_ps = psum_t.tile([P, 2 * C_PASSES, P], F32, tag="tp")
+                w_ps = pool.tile([P, 2 * C_PASSES, P], F32, tag=tag)
                 for j in range(2 * C_PASSES):
                     nc.tensor.transpose(
-                        w_ps[:, j, :], w_rows[ge, t][:].bitcast(F32)[:, P * j : P * j + P], ident_f32[:]
+                        w_ps[:, j, :], w_rows[ge][:, t, :].bitcast(F32)[:, P * j : P * j + P], ident_f32[:]
                     )
                 dst = words[:, :, P * t : P * t + P, :]
                 src = w_ps[:].rearrange("p (g u) e -> p g e u", u=2)
@@ -142,7 +138,7 @@ def tile_attentionlayer_pa_kernel(
             )
 
         def transpose_x(n, pool, tag):
-            grouped = work.tile([P, C_PASSES * TQ * PACK], BF16, align_bytes=64, name="x_grouped", bufs=1)
+            grouped = work.tile([P, C_PASSES * TQ * PACK], BF16, align_bytes=64, tag="grouped", bufs=3, name="x_grouped")
             words = grouped[:].bitcast(F32).rearrange("p (g q u) -> p g q u", g=C_PASSES, u=2)
             for r in range(Q_TILES):
                 x_ps = pool.tile([P, 2 * C_PASSES, P], F32, tag=tag)
@@ -165,65 +161,59 @@ def tile_attentionlayer_pa_kernel(
             )
             x_codes[n], x_scales[n] = codes, scales
 
-        def regrouped_views(grouped, n, ge, sh):
-            chunk = k_sb[n, ge][:, :, N_MOVE * sh : N_MOVE * sh + N_MOVE]
+        def regrouped_views(grouped, n, ge, cols):
             return (
-                grouped[:].rearrange("p (c i) t -> p c t i", i=4),
-                chunk.rearrange("p t (c i) -> p c t i", i=4),
+                grouped[:, cols, :].rearrange("p (c i) t -> p c t i", i=4),
+                k_sb[n, ge][:, :, cols].rearrange("p t (c i) -> p c t i", i=4),
             )
 
-        def regroup_on_scalar(n):
-            ge, sh = SCALAR_CHUNK
-            k_grouped_s = work.tile([P, N_MOVE, PACK], BF16, align_bytes=64)
-            dst, src = regrouped_views(k_grouped_s, n, ge, sh)
-            nc.scalar.copy(out=dst, in_=src)
-            k_from_scalar[n] = k_grouped_s
+        def new_last_pass(n):
+            grouped = work.tile([P, TS, PACK], BF16, align_bytes=64, name="k_grouped_last")
+            k_grouped[n, E_PASSES - 1] = grouped
 
-        def regroup_on_vector(n, ge, sh):
-            k_grouped = work.tile([P, N_MOVE, PACK], BF16, align_bytes=64, bufs=3)
-            dst, src = regrouped_views(k_grouped, n, ge, sh)
-            nc.vector.tensor_copy(out=dst, in_=src)
-            return k_grouped
+        def regroup_on_scalar(n):
+            new_last_pass(n)
+            dst, src = regrouped_views(k_grouped[n, E_PASSES - 1], n, E_PASSES - 1, slice(SCALAR_FROM, TS))
+            nc.scalar.copy(out=dst, in_=src)
 
         def regroup_on_gpsimd(n):
-            ge, sh = GPSIMD_CHUNK
             go = work.tile([P, 1], F32)
             nc.vector.memset(go[:], 1.0)
-            k_grouped_g = work.tile([P, N_MOVE, PACK], BF16, align_bytes=64, bufs=1)
+            cols = slice(0, SCALAR_FROM)
             nc.gpsimd.tensor_scalar(
-                out=k_grouped_g[:],
-                in0=k_sb[n, ge][:, :, N_MOVE * sh : N_MOVE * sh + N_MOVE].rearrange("p t c -> p c t"),
+                out=k_grouped[n, E_PASSES - 1][:, cols, :],
+                in0=k_sb[n, E_PASSES - 1][:, :, cols].rearrange("p t c -> p c t"),
                 scalar1=go[:],
                 scalar2=0.0,
                 op0=ALU.mult,
                 op1=ALU.add,
             )
-            k_from_gpsimd[n] = k_grouped_g
 
-        def quantise_chunk(n, ge, sh, grouped):
-            s_cols = slice(N_MOVE * sh, N_MOVE * sh + N_MOVE)
+        def regroup_pass_on_vector(n, ge):
+            for sh in range(S_HALVES):
+                dst, src = regrouped_views(k_grouped[n, ge], n, ge, slice(N_MOVE * sh, N_MOVE * sh + N_MOVE))
+                nc.vector.tensor_copy(out=dst, in_=src)
+
+        def regroup_first_pass(n):
+            grouped = work.tile([P, TS, PACK], BF16, align_bytes=64, name="k_grouped_first", bufs=1)
+            k_grouped[n, 0] = grouped
+            regroup_pass_on_vector(n, 0)
+
+        def quantise_pass(n, ge):
             nc.vector.quantize_mx(
-                out=k_codes[n][:, ge, s_cols].bitcast(FP8X4),
-                scales=k_scales[n][:, ge, s_cols],
-                in_=grouped[:].rearrange("p s t -> p (s t)"),
+                out=k_codes[n][:, ge, :].bitcast(FP8X4),
+                scales=k_scales[n][:, ge, :],
+                in_=k_grouped[n, ge][:].rearrange("p s t -> p (s t)"),
             )
 
-        def quantise_keys(n, x_batch):
+        def new_key_codes(n):
             codes = work.tile([P, E_PASSES, TS], U32, align_bytes=64, name="k_codes")
             scales = work.tile([P, E_PASSES, TS], U8, align_bytes=64, name="k_scales")
             k_codes[n], k_scales[n] = codes, scales
-            chunk_00 = regroup_on_vector(n, 0, 0)
-            chunk_01 = regroup_on_vector(n, 0, 1)
-            quantise_chunk(n, 0, 0, chunk_00)
-            chunk_10 = k_from_gpsimd[n] if n in k_from_gpsimd else regroup_on_vector(n, 1, 0)
-            quantise_chunk(n, 0, 1, chunk_01)
-            if x_batch < BATCH:
-                quantise_x(x_batch)
-            quantise_chunk(n, 1, 0, chunk_10)
 
-        def project(n):
-            for ge in range(E_PASSES):
-                part = work.tile([P, PACK, TQ], F32, name="h_part")
+        def project(n, passes=range(E_PASSES)):
+            for ge in passes:
+                part = work.tile([P, PACK, TQ], F32, tag="rows_or_part", bufs=4)
                 for t in range(PACK):
                     h_ps = psum_mx.tile([P, TQ], F32, tag="mx")
                     for gc in range(C_PASSES):
@@ -254,45 +244,57 @@ def tile_attentionlayer_pa_kernel(
                             )
                     te_ps[n, ge, hq] = bank
 
-        def finish_h(n, x_batch=BATCH):
-            codes = work.tile([P, 2, E_PASSES, Q_HALF], U32, align_bytes=64, name="h_codes")
-            scales = work.tile([P, 2, E_PASSES, Q_HALF], U8, align_bytes=64, name="h_scales")
+        def finish_h(n, pieces):
+            width = TQ // pieces
+            span = E_PASSES * width
+            codes = work.tile([P, E_PASSES * TQ], U32, align_bytes=64, name="h_codes")
+            scales = work.tile([P, E_PASSES * TQ], U8, align_bytes=64, name="h_scales")
             grouped = {}
             for hq in range(2):
-                h_grouped = work.tile([P, E_PASSES, Q_HALF, PACK], BF16, align_bytes=64)
+                h_grouped = work.tile([P, E_PASSES * Q_HALF, PACK], BF16, align_bytes=64)
                 grouped[hq] = h_grouped
 
-            def add_embedding(hq, ge):
-                q_cols = slice(Q_HALF * hq, Q_HALF * hq + Q_HALF)
+            def piece_of_half(i):
+                hq, j = divmod(i, pieces // 2)
+                return hq, j, grouped[hq][:, span * j : span * j + span, :]
+
+            def add_embedding(i, ge):
+                hq, j, piece = piece_of_half(i)
+                in_half = slice(width * j, width * j + width)
                 nc.vector.scalar_tensor_tensor(
-                    out=grouped[hq][:, ge],
-                    in0=te_ps[n, ge, hq][:].rearrange("p t q -> p q t"),
+                    out=piece[:, width * ge : width * ge + width, :],
+                    in0=te_ps[n, ge, hq][:, :, in_half].rearrange("p t q -> p q t"),
                     scalar=SQRT_HALF,
-                    in1=h_part[n, ge][:, :, q_cols].rearrange("p t q -> p q t"),
+                    in1=h_part[n, ge][:, :, width * i : width * i + width].rearrange("p t q -> p q t"),
                     op0=ALU.mult,
                     op1=ALU.add,
                 )
 
-            def quantise_half(hq):
+            def quantise_piece(i):
+                hq, j, piece = piece_of_half(i)
                 nc.vector.quantize_mx(
-                    out=codes[:, hq].rearrange("p g q -> p (g q)").bitcast(FP8X4),
-                    scales=scales[:, hq].rearrange("p g q -> p (g q)"),
-                    in_=grouped[hq][:].rearrange("p g q t -> p (g q t)"),
+                    out=codes[:, span * i : span * i + span].bitcast(FP8X4),
+                    scales=scales[:, span * i : span * i + span],
+                    in_=piece.rearrange("p q t -> p (q t)"),
                 )
 
-            for hq in range(2):
+            for i in range(pieces):
+                add_embedding(i, 0)
+                if 0 < i < pieces - 1:
+                    quantise_piece(i - 1)
+                add_embedding(i, 1)
+            quantise_piece(pieces - 2)
+            quantise_piece(pieces - 1)
+            for r in range(Q_TILES):
+                i, off = divmod(P * r, width)
                 for ge in range(E_PASSES):
-                    add_embedding(hq, ge)
-            if x_batch < BATCH:
-                quantise_x(x_batch)
-            quantise_half(0)
-            quantise_half(1)
+                    first = span * i + width * ge + off
+                    h_cols[n, r, ge] = slice(first, first + P)
             h_codes[n], h_scales[n] = codes, scales
 
         def scores(n, vector_helps):
             out_rows = out[n].rearrange("(p r) s -> p r s", r=Q_TILES)
             for r in range(Q_TILES):
-                hq, rr = divmod(r, 2)
                 o_sb = work.tile([P, TS], F32, bufs=4)
                 for sh in range(S_HALVES):
                     s_cols = slice(N_MOVE * sh, N_MOVE * sh + N_MOVE)
@@ -300,14 +302,14 @@ def tile_attentionlayer_pa_kernel(
                     for ge in range(E_PASSES):
                         nc.tensor.matmul_mx(
                             out=o_ps[:],
-                            lhsT=h_codes[n][:, hq, ge, P * rr : P * rr + P].bitcast(FP8X4),
-                            lhsT_scale=h_scales[n][:, hq, ge, P * rr : P * rr + P],
+                            lhsT=h_codes[n][:, h_cols[n, r, ge]].bitcast(FP8X4),
+                            lhsT_scale=h_scales[n][:, h_cols[n, r, ge]],
                             rhs=k_codes[n][:, ge, s_cols].bitcast(FP8X4),
                             rhs_scale=k_scales[n][:, ge, s_cols],
                             start=(ge == 0),
                             stop=(ge == E_PASSES - 1),
                         )
-                    if vector_helps and sh == 1:
+                    if vector_helps and r >= 2 and sh == 1:
                         nc.vector.tensor_copy(out=o_sb[:, s_cols], in_=o_ps[:])
                     else:
                         nc.scalar.copy(out=o_sb[:, s_cols], in_=o_ps[:])
@@ -315,8 +317,13 @@ def tile_attentionlayer_pa_kernel(
 
         for ge in range(E_PASSES):
             load_v(ge)
-        load_batch(0)
-        load_batch(1)
+        load_x(0)
+        load_te(0)
+        load_keys(0)
+        load_x(1)
+        load_keys(1)
+        load_x(2)
+        load_te(1)
 
         gb_rows = const.tile([P, P], BF16)
         nc.vector.memset(gb_rows[:], 0.0)
@@ -362,6 +369,8 @@ def tile_attentionlayer_pa_kernel(
         sum_squares(1, 3)
         times_gain(0)
         norm_columns(1)
+        new_w_rows(0)
+        new_w_rows(1)
         scale_rows(0, 0)
         scale_rows(0, 1)
         invert_norm(1)
@@ -371,35 +380,46 @@ def tile_attentionlayer_pa_kernel(
         for t in range(PACK):
             scale_rows(1, t)
         transpose_x(0, pool=psum_mx, tag="mx")
-        transpose_w(0)
+        transpose_w(0, pool=psum_t, tag="tp")
         quantise_x(0)
         quantise_w(0)
-        transpose_w(1)
-        quantise_w(1)
-        project(0)
+        transpose_w(1, pool=psum_mx, tag="mx")
         transpose_te(0)
+        quantise_w(1)
+        project(0, passes=(0,))
         transpose_x(1, pool=psum_mx, tag="mx")
-        regroup_on_scalar(0)
+        project(0, passes=(1,))
+        new_key_codes(0)
+        regroup_first_pass(0)
+        new_last_pass(0)
+        regroup_pass_on_vector(0, E_PASSES - 1)
+        quantise_x(1)
+        quantise_pass(0, 0)
         regroup_on_scalar(1)
-        quantise_keys(0, x_batch=BATCH)
 
         for n in range(BATCH):
             if n + 2 < BATCH:
-                load_batch(n + 2)
+                load_keys(n + 2)
+                if n + 3 < BATCH:
+                    load_x(n + 3)
+                load_te(n + 2)
             if n + 1 < BATCH:
                 regroup_on_gpsimd(n + 1)
-            finish_h(n, x_batch=1 if n == 0 else BATCH)
+            finish_h(n, pieces=4 if n == BATCH - 1 else 2)
             if n == 0:
-                quantise_chunk(0, *SCALAR_CHUNK, k_from_scalar[0])
-            if n >= 1:
-                scores(n - 1, vector_helps=False)
-            if n + 2 < BATCH:
-                transpose_x(n + 2, pool=psum_t, tag="tp")
+                quantise_pass(0, E_PASSES - 1)
             if n + 1 < BATCH:
                 project(n + 1)
-                transpose_te(n + 1)
-                quantise_keys(n + 1, x_batch=n + 2)
-                quantise_chunk(n + 1, *SCALAR_CHUNK, k_from_scalar[n + 1])
             if n + 2 < BATCH:
+                transpose_x(n + 2, pool=psum_t, tag="tp")
                 regroup_on_scalar(n + 2)
+            if n + 1 < BATCH:
+                transpose_te(n + 1)
+                scores(n, vector_helps=False)
+                new_key_codes(n + 1)
+                regroup_first_pass(n + 1)
+                if n + 2 < BATCH:
+                    quantise_x(n + 2)
+                quantise_pass(n + 1, E_PASSES - 1)
+                quantise_pass(n + 1, 0)
         scores(BATCH - 1, vector_helps=True)

@@ -60,12 +60,11 @@ def tile_attentionlayer_pa_kernel(
             nc.sync.dma_start(out=x_tile[:], in_=x[n].rearrange("(p r) c -> p r c", r=Q_TILES))
             x_sb[n] = x_tile
 
-        def load_keys(n):
-            for ge in range(E_PASSES):
-                k_tile = raw.tile([P, PACK, TS], BF16, tag="raw")
-                rows = encoder_keys[n][K_PASS * ge : K_PASS * ge + K_PASS, :]
-                nc.sync.dma_start(out=k_tile[:], in_=rows.rearrange("(t p) s -> p t s", p=P))
-                k_sb[n, ge] = k_tile
+        def load_keys(n, ge):
+            k_tile = raw.tile([P, PACK, TS], BF16, tag="raw")
+            rows = encoder_keys[n][K_PASS * ge : K_PASS * ge + K_PASS, :]
+            nc.sync.dma_start(out=k_tile[:], in_=rows.rearrange("(t p) s -> p t s", p=P))
+            k_sb[n, ge] = k_tile
 
         def load_te(n):
             te_tile = raw.tile([P, Q_TILES, E], BF16, tag="raw")
@@ -124,7 +123,7 @@ def tile_attentionlayer_pa_kernel(
                     )
                 dst = words[:, :, P * t : P * t + P, :]
                 src = w_ps[:].rearrange("p (g u) e -> p g e u", u=2)
-                if t % 2 == 0:
+                if ge == 0 and t % 2 == 0:
                     nc.vector.tensor_copy(out=dst, in_=src)
                 else:
                     nc.scalar.copy(out=dst, in_=src)
@@ -172,7 +171,6 @@ def tile_attentionlayer_pa_kernel(
             k_grouped[n, E_PASSES - 1] = grouped
 
         def regroup_on_scalar(n):
-            new_last_pass(n)
             dst, src = regrouped_views(k_grouped[n, E_PASSES - 1], n, E_PASSES - 1, slice(SCALAR_FROM, TS))
             nc.scalar.copy(out=dst, in_=src)
 
@@ -189,15 +187,17 @@ def tile_attentionlayer_pa_kernel(
                 op1=ALU.add,
             )
 
-        def regroup_pass_on_vector(n, ge):
-            for sh in range(S_HALVES):
-                dst, src = regrouped_views(k_grouped[n, ge], n, ge, slice(N_MOVE * sh, N_MOVE * sh + N_MOVE))
-                nc.vector.tensor_copy(out=dst, in_=src)
-
-        def regroup_first_pass(n):
+        def new_first_pass(n):
             grouped = work.tile([P, TS, PACK], BF16, align_bytes=64, name="k_grouped_first", bufs=1)
             k_grouped[n, 0] = grouped
-            regroup_pass_on_vector(n, 0)
+
+        def regroup_half(n, ge, sh, copy):
+            dst, src = regrouped_views(k_grouped[n, ge], n, ge, slice(N_MOVE * sh, N_MOVE * sh + N_MOVE))
+            copy(out=dst, in_=src)
+
+        def regroup_pass_on_vector(n, ge):
+            for sh in range(S_HALVES):
+                regroup_half(n, ge, sh, nc.vector.tensor_copy)
 
         def quantise_pass(n, ge):
             nc.vector.quantize_mx(
@@ -319,10 +319,12 @@ def tile_attentionlayer_pa_kernel(
             load_v(ge)
         load_x(0)
         load_te(0)
-        load_keys(0)
+        load_keys(0, 0)
+        load_keys(0, 1)
         load_x(1)
-        load_keys(1)
+        load_keys(1, 1)
         load_x(2)
+        load_keys(1, 0)
         load_te(1)
 
         gb_rows = const.tile([P, P], BF16)
@@ -386,24 +388,27 @@ def tile_attentionlayer_pa_kernel(
         transpose_w(1, pool=psum_mx, tag="mx")
         transpose_te(0)
         quantise_w(1)
+        new_first_pass(0)
+        regroup_half(0, 0, 1, nc.scalar.copy)
         project(0, passes=(0,))
         transpose_x(1, pool=psum_mx, tag="mx")
         project(0, passes=(1,))
         new_key_codes(0)
-        regroup_first_pass(0)
+        regroup_half(0, 0, 0, nc.vector.tensor_copy)
         new_last_pass(0)
         regroup_pass_on_vector(0, E_PASSES - 1)
-        quantise_x(1)
         quantise_pass(0, 0)
-        regroup_on_scalar(1)
+        quantise_x(1)
 
         for n in range(BATCH):
             if n + 2 < BATCH:
-                load_keys(n + 2)
+                load_keys(n + 2, 1)
                 if n + 3 < BATCH:
                     load_x(n + 3)
+                load_keys(n + 2, 0)
                 load_te(n + 2)
             if n + 1 < BATCH:
+                new_last_pass(n + 1)
                 regroup_on_gpsimd(n + 1)
             finish_h(n, pieces=4 if n == BATCH - 1 else 2)
             if n == 0:
@@ -412,14 +417,18 @@ def tile_attentionlayer_pa_kernel(
                 project(n + 1)
             if n + 2 < BATCH:
                 transpose_x(n + 2, pool=psum_t, tag="tp")
-                regroup_on_scalar(n + 2)
             if n + 1 < BATCH:
+                regroup_on_scalar(n + 1)
                 transpose_te(n + 1)
                 scores(n, vector_helps=False)
                 new_key_codes(n + 1)
-                regroup_first_pass(n + 1)
+                new_first_pass(n + 1)
+                regroup_pass_on_vector(n + 1, 0)
                 if n + 2 < BATCH:
                     quantise_x(n + 2)
-                quantise_pass(n + 1, E_PASSES - 1)
-                quantise_pass(n + 1, 0)
+                    quantise_pass(n + 1, 0)
+                    quantise_pass(n + 1, E_PASSES - 1)
+                else:
+                    quantise_pass(n + 1, E_PASSES - 1)
+                    quantise_pass(n + 1, 0)
         scores(BATCH - 1, vector_helps=True)

@@ -136,6 +136,13 @@ def tile_attentionlayer_pa_kernel(
                 in_=w_grouped[ge][:],
             )
 
+        def busy_matmuls(count, ge, t, pool, tag):
+            unread = pool.tile([P, N_MOVE], F32, tag=tag)
+            for j in range(count):
+                nc.tensor.matmul(
+                    unread[:], lhsT=v_sb[ge][:, t, 0:P], rhs=v_sb[ge][:, t, 0:N_MOVE], start=True, stop=True
+                )
+
         def transpose_x(n, pool, tag):
             grouped = work.tile([P, C_PASSES * TQ * PACK], BF16, align_bytes=64, tag="grouped", bufs=3, name="x_grouped")
             words = grouped[:].bitcast(F32).rearrange("p (g q u) -> p g q u", g=C_PASSES, u=2)
@@ -292,9 +299,9 @@ def tile_attentionlayer_pa_kernel(
                     h_cols[n, r, ge] = slice(first, first + P)
             h_codes[n], h_scales[n] = codes, scales
 
-        def scores(n, vector_helps):
+        def scores(n, vector_helps, row_tiles=range(Q_TILES)):
             out_rows = out[n].rearrange("(p r) s -> p r s", r=Q_TILES)
-            for r in range(Q_TILES):
+            for r in row_tiles:
                 o_sb = work.tile([P, TS], F32, bufs=4)
                 for sh in range(S_HALVES):
                     s_cols = slice(N_MOVE * sh, N_MOVE * sh + N_MOVE)
@@ -381,11 +388,16 @@ def tile_attentionlayer_pa_kernel(
         scale_rows(0, 3)
         for t in range(PACK):
             scale_rows(1, t)
+        for t in range(PACK):
+            busy_matmuls(2, 1, t, pool=psum_t, tag="tp")
         transpose_x(0, pool=psum_mx, tag="mx")
+        busy_matmuls(2, 1, 3, pool=psum_t, tag="tp")
         transpose_w(0, pool=psum_t, tag="tp")
         quantise_x(0)
         quantise_w(0)
+        busy_matmuls(2, 1, 3, pool=psum_mx, tag="mx")
         transpose_w(1, pool=psum_mx, tag="mx")
+        busy_matmuls(2, 1, 3, pool=psum_t, tag="tp")
         transpose_te(0)
         quantise_w(1)
         new_first_pass(0)
@@ -419,8 +431,9 @@ def tile_attentionlayer_pa_kernel(
                 transpose_x(n + 2, pool=psum_t, tag="tp")
             if n + 1 < BATCH:
                 regroup_on_scalar(n + 1)
+                scores(n, vector_helps=False, row_tiles=(0, 1))
                 transpose_te(n + 1)
-                scores(n, vector_helps=False)
+                scores(n, vector_helps=False, row_tiles=(2, 3))
                 new_key_codes(n + 1)
                 new_first_pass(n + 1)
                 regroup_pass_on_vector(n + 1, 0)

@@ -98,10 +98,6 @@ def tile_attentionlayer_pa_kernel(
             cols = slice(PACK * ge, PACK * ge + PACK)
             nc.vector.reciprocal(out=inv_norm[:, cols], in_=norm[:, cols])
 
-        def times_gain(ge):
-            cols = slice(PACK * ge, PACK * ge + PACK)
-            nc.vector.tensor_mul(out=row_scale[:, cols], in0=inv_norm[:, cols], in1=gain[:, cols])
-
         def new_w_rows(ge):
             rows = work.tile([P, PACK, C], BF16, tag="rows_or_part", bufs=4)
             w_rows[ge] = rows
@@ -109,7 +105,12 @@ def tile_attentionlayer_pa_kernel(
         def scale_rows(ge, t):
             m = PACK * ge + t
             nc.vector.tensor_scalar(
-                out=w_rows[ge][:, t, :], in0=v_sb[ge][:, t, :], scalar1=row_scale[:, m : m + 1], scalar2=None, op0=ALU.mult
+                out=w_rows[ge][:, t, :],
+                in0=v_sb[ge][:, t, :],
+                scalar1=inv_norm[:, m : m + 1],
+                scalar2=gain[:, m : m + 1],
+                op0=ALU.mult,
+                op1=ALU.mult,
             )
 
         def transpose_w(ge, pool, tag):
@@ -178,8 +179,8 @@ def tile_attentionlayer_pa_kernel(
             k_grouped[n, E_PASSES - 1] = grouped
 
         def regroup_on_scalar(n):
-            dst, src = regrouped_views(k_grouped[n, E_PASSES - 1], n, E_PASSES - 1, slice(SCALAR_FROM, TS))
-            nc.scalar.copy(out=dst, in_=src)
+            for ge in range(E_PASSES):
+                regroup(n, ge, slice(SCALAR_FROM, TS), nc.scalar.copy)
 
         def regroup_on_gpsimd(n):
             go = work.tile([P, 1], F32)
@@ -198,13 +199,9 @@ def tile_attentionlayer_pa_kernel(
             grouped = work.tile([P, TS, PACK], BF16, align_bytes=64, name="k_grouped_first", bufs=1)
             k_grouped[n, 0] = grouped
 
-        def regroup_half(n, ge, sh, copy):
-            dst, src = regrouped_views(k_grouped[n, ge], n, ge, slice(N_MOVE * sh, N_MOVE * sh + N_MOVE))
+        def regroup(n, ge, cols, copy):
+            dst, src = regrouped_views(k_grouped[n, ge], n, ge, cols)
             copy(out=dst, in_=src)
-
-        def regroup_pass_on_vector(n, ge):
-            for sh in range(S_HALVES):
-                regroup_half(n, ge, sh, nc.vector.tensor_copy)
 
         def quantise_pass(n, ge):
             nc.vector.quantize_mx(
@@ -362,21 +359,17 @@ def tile_attentionlayer_pa_kernel(
         sumsq = const.tile([P, E_TILES], F32)
         norm = const.tile([P, E_TILES], F32)
         inv_norm = const.tile([P, E_TILES], F32)
-        row_scale = const.tile([P, E_TILES], F32)
 
         for t in range(PACK):
             sum_squares(0, t)
         sum_squares(1, 0)
         sum_squares(1, 1)
         norm_columns(0)
-        nc.vector.tensor_copy(out=gain[:], in_=gb_ps[:, 0:E_TILES])
-        nc.vector.tensor_scalar(
-            out=bias_s[:], in0=gb_ps[:, E_TILES : 2 * E_TILES], scalar1=SQRT_HALF, scalar2=None, op0=ALU.mult
-        )
+        nc.scalar.copy(out=gain[:], in_=gb_ps[:, 0:E_TILES])
+        nc.scalar.mul(bias_s[:], gb_ps[:, E_TILES : 2 * E_TILES], SQRT_HALF)
         sum_squares(1, 2)
         invert_norm(0)
         sum_squares(1, 3)
-        times_gain(0)
         norm_columns(1)
         new_w_rows(0)
         new_w_rows(1)
@@ -384,7 +377,6 @@ def tile_attentionlayer_pa_kernel(
         scale_rows(0, 1)
         invert_norm(1)
         scale_rows(0, 2)
-        times_gain(1)
         scale_rows(0, 3)
         for t in range(PACK):
             scale_rows(1, t)
@@ -401,14 +393,14 @@ def tile_attentionlayer_pa_kernel(
         transpose_te(0)
         quantise_w(1)
         new_first_pass(0)
-        regroup_half(0, 0, 1, nc.scalar.copy)
+        regroup(0, 0, slice(N_MOVE, TS), nc.scalar.copy)
         project(0, passes=(0,))
         transpose_x(1, pool=psum_mx, tag="mx")
         project(0, passes=(1,))
         new_key_codes(0)
-        regroup_half(0, 0, 0, nc.vector.tensor_copy)
+        regroup(0, 0, slice(0, N_MOVE), nc.vector.tensor_copy)
         new_last_pass(0)
-        regroup_pass_on_vector(0, E_PASSES - 1)
+        regroup(0, E_PASSES - 1, slice(0, TS), nc.vector.tensor_copy)
         quantise_pass(0, 0)
         quantise_x(1)
 
@@ -430,13 +422,13 @@ def tile_attentionlayer_pa_kernel(
             if n + 2 < BATCH:
                 transpose_x(n + 2, pool=psum_t, tag="tp")
             if n + 1 < BATCH:
+                new_first_pass(n + 1)
                 regroup_on_scalar(n + 1)
                 scores(n, vector_helps=False, row_tiles=(0, 1))
                 transpose_te(n + 1)
                 scores(n, vector_helps=False, row_tiles=(2, 3))
                 new_key_codes(n + 1)
-                new_first_pass(n + 1)
-                regroup_pass_on_vector(n + 1, 0)
+                regroup(n + 1, 0, slice(0, SCALAR_FROM), nc.vector.tensor_copy)
                 if n + 2 < BATCH:
                     quantise_x(n + 2)
                     quantise_pass(n + 1, 0)

@@ -178,17 +178,12 @@ def tile_attentionlayer_pa_kernel(
             grouped = work.tile([P, TS, PACK], BF16, align_bytes=64, name="k_grouped_last")
             k_grouped[n, E_PASSES - 1] = grouped
 
-        def regroup_on_scalar(n):
-            for ge in range(E_PASSES):
-                regroup(n, ge, slice(SCALAR_FROM, TS), nc.scalar.copy)
-
         def regroup_on_gpsimd(n):
             go = work.tile([P, 1], F32)
             nc.vector.memset(go[:], 1.0)
-            cols = slice(0, SCALAR_FROM)
             nc.gpsimd.tensor_scalar(
-                out=k_grouped[n, E_PASSES - 1][:, cols, :],
-                in0=k_sb[n, E_PASSES - 1][:, :, cols].rearrange("p t c -> p c t"),
+                out=k_grouped[n, E_PASSES - 1][:],
+                in0=k_sb[n, E_PASSES - 1][:].rearrange("p t c -> p c t"),
                 scalar1=go[:],
                 scalar2=0.0,
                 op0=ALU.mult,
@@ -296,9 +291,9 @@ def tile_attentionlayer_pa_kernel(
                     h_cols[n, r, ge] = slice(first, first + P)
             h_codes[n], h_scales[n] = codes, scales
 
-        def scores(n, vector_helps, row_tiles=range(Q_TILES)):
+        def scores(n, vector_helps):
             out_rows = out[n].rearrange("(p r) s -> p r s", r=Q_TILES)
-            for r in row_tiles:
+            for r in range(Q_TILES):
                 o_sb = work.tile([P, TS], F32, bufs=4)
                 for sh in range(S_HALVES):
                     s_cols = slice(N_MOVE * sh, N_MOVE * sh + N_MOVE)
@@ -423,10 +418,9 @@ def tile_attentionlayer_pa_kernel(
                 transpose_x(n + 2, pool=psum_t, tag="tp")
             if n + 1 < BATCH:
                 new_first_pass(n + 1)
-                regroup_on_scalar(n + 1)
-                scores(n, vector_helps=False, row_tiles=(0, 1))
+                regroup(n + 1, 0, slice(SCALAR_FROM, TS), nc.scalar.copy)
                 transpose_te(n + 1)
-                scores(n, vector_helps=False, row_tiles=(2, 3))
+                scores(n, vector_helps=False)
                 new_key_codes(n + 1)
                 regroup(n + 1, 0, slice(0, SCALAR_FROM), nc.vector.tensor_copy)
                 if n + 2 < BATCH:

@@ -279,10 +279,11 @@ def tile_attentionlayer_pa_kernel(
 
             for i in range(pieces):
                 add_embedding(i, 0)
-                if 0 < i < pieces - 1:
+                if pieces > 2 and i > 0:
                     quantise_piece(i - 1)
                 add_embedding(i, 1)
-            quantise_piece(pieces - 2)
+            if pieces == 2:
+                quantise_piece(0)
             quantise_piece(pieces - 1)
             for r in range(Q_TILES):
                 i, off = divmod(P * r, width)
@@ -423,11 +424,8 @@ def tile_attentionlayer_pa_kernel(
                 scores(n, vector_helps=False)
                 new_key_codes(n + 1)
                 regroup(n + 1, 0, slice(0, SCALAR_FROM), nc.vector.tensor_copy)
+                quantise_pass(n + 1, E_PASSES - 1)
                 if n + 2 < BATCH:
                     quantise_x(n + 2)
-                    quantise_pass(n + 1, 0)
-                    quantise_pass(n + 1, E_PASSES - 1)
-                else:
-                    quantise_pass(n + 1, E_PASSES - 1)
-                    quantise_pass(n + 1, 0)
+                quantise_pass(n + 1, 0)
         scores(BATCH - 1, vector_helps=True)

@@ -25,7 +25,8 @@ Q_TILES = TQ // P
 Q_HALF = TQ // 2
 S_HALVES = TS // N_MOVE
 SQRT_HALF = math.sqrt(0.5)
-SCALAR_FROM = 768
+SCALAR_FROM = (512, 768, 768, 512)
+SCALAR_SQUARES = 576
 
 FLOPS = 2 * BATCH * TQ * C * E + 2 * BATCH * TQ * E * TS
 
@@ -72,26 +73,28 @@ def tile_attentionlayer_pa_kernel(
             te_sb[n] = te_tile
 
         def sum_squares(ge, t):
-            half = C // 2
             m = PACK * ge + t
-            squares_s = work.tile([P, half], BF16, bufs=1)
+            squares_s = work.tile([P, SCALAR_SQUARES], BF16, bufs=1)
             nc.scalar.activation(
-                out=squares_s[:], in_=v_sb[ge][:, t, 0:half], func=ACT.Square, accum_out=sumsq_s[:, m : m + 1]
+                out=squares_s[:], in_=v_sb[ge][:, t, 0:SCALAR_SQUARES], func=ACT.Square, accum_out=sumsq_s[:, m : m + 1]
             )
-            squares_v = work.tile([P, half], F32, bufs=1)
+            squares_v = work.tile([P, C - SCALAR_SQUARES], F32, bufs=1)
             nc.vector.scalar_tensor_tensor(
                 out=squares_v[:],
-                in0=v_sb[ge][:, t, half:C],
+                in0=v_sb[ge][:, t, SCALAR_SQUARES:C],
                 scalar=1.0,
-                in1=v_sb[ge][:, t, half:C],
+                in1=v_sb[ge][:, t, SCALAR_SQUARES:C],
                 op0=ALU.mult,
                 op1=ALU.mult,
                 accum_out=sumsq_v[:, m : m + 1],
             )
 
-        def norm_columns(ge):
+        def add_sums(ge):
             cols = slice(PACK * ge, PACK * ge + PACK)
             nc.vector.tensor_add(out=sumsq[:, cols], in0=sumsq_s[:, cols], in1=sumsq_v[:, cols])
+
+        def take_root(ge):
+            cols = slice(PACK * ge, PACK * ge + PACK)
             nc.scalar.activation(out=norm[:, cols], in_=sumsq[:, cols], func=ACT.Sqrt)
 
         def invert_norm(ge):
@@ -282,6 +285,8 @@ def tile_attentionlayer_pa_kernel(
                 if pieces > 2 and i > 0:
                     quantise_piece(i - 1)
                 add_embedding(i, 1)
+                if pieces > 2 and i == 0:
+                    quantise_pass(n, 0)
             if pieces == 2:
                 quantise_piece(0)
             quantise_piece(pieces - 1)
@@ -359,14 +364,16 @@ def tile_attentionlayer_pa_kernel(
         for t in range(PACK):
             sum_squares(0, t)
         sum_squares(1, 0)
-        sum_squares(1, 1)
-        norm_columns(0)
         nc.scalar.copy(out=gain[:], in_=gb_ps[:, 0:E_TILES])
         nc.scalar.mul(bias_s[:], gb_ps[:, E_TILES : 2 * E_TILES], SQRT_HALF)
+        sum_squares(1, 1)
+        add_sums(0)
         sum_squares(1, 2)
-        invert_norm(0)
+        take_root(0)
         sum_squares(1, 3)
-        norm_columns(1)
+        invert_norm(0)
+        add_sums(1)
+        take_root(1)
         new_w_rows(0)
         new_w_rows(1)
         scale_rows(0, 0)
@@ -389,12 +396,12 @@ def tile_attentionlayer_pa_kernel(
         transpose_te(0)
         quantise_w(1)
         new_first_pass(0)
-        regroup(0, 0, slice(N_MOVE, TS), nc.scalar.copy)
+        regroup(0, 0, slice(SCALAR_FROM[0], TS), nc.scalar.copy)
         project(0, passes=(0,))
         transpose_x(1, pool=psum_mx, tag="mx")
         project(0, passes=(1,))
         new_key_codes(0)
-        regroup(0, 0, slice(0, N_MOVE), nc.vector.tensor_copy)
+        regroup(0, 0, slice(0, SCALAR_FROM[0]), nc.vector.tensor_copy)
         new_last_pass(0)
         regroup(0, E_PASSES - 1, slice(0, TS), nc.vector.tensor_copy)
         quantise_pass(0, 0)
@@ -419,13 +426,13 @@ def tile_attentionlayer_pa_kernel(
                 transpose_x(n + 2, pool=psum_t, tag="tp")
             if n + 1 < BATCH:
                 new_first_pass(n + 1)
-                regroup(n + 1, 0, slice(SCALAR_FROM, TS), nc.scalar.copy)
+                regroup(n + 1, 0, slice(SCALAR_FROM[n + 1], TS), nc.scalar.copy)
                 transpose_te(n + 1)
                 scores(n, vector_helps=False)
                 new_key_codes(n + 1)
-                regroup(n + 1, 0, slice(0, SCALAR_FROM), nc.vector.tensor_copy)
+                regroup(n + 1, 0, slice(0, SCALAR_FROM[n + 1]), nc.vector.tensor_copy)
                 quantise_pass(n + 1, E_PASSES - 1)
                 if n + 2 < BATCH:
                     quantise_x(n + 2)
-                quantise_pass(n + 1, 0)
+                    quantise_pass(n + 1, 0)
         scores(BATCH - 1, vector_helps=True)

@@ -26,6 +26,7 @@ Q_HALF = TQ // 2
 S_HALVES = TS // N_MOVE
 SQRT_HALF = math.sqrt(0.5)
 SCALAR_FROM = (512, 768, 768, 512)
+GPSIMD_TO = 896
 SCALAR_SQUARES = 576
 
 FLOPS = 2 * BATCH * TQ * C * E + 2 * BATCH * TQ * E * TS
@@ -184,9 +185,10 @@ def tile_attentionlayer_pa_kernel(
         def regroup_on_gpsimd(n):
             go = work.tile([P, 1], F32)
             nc.vector.memset(go[:], 1.0)
+            cols = slice(0, GPSIMD_TO)
             nc.gpsimd.tensor_scalar(
-                out=k_grouped[n, E_PASSES - 1][:],
-                in0=k_sb[n, E_PASSES - 1][:].rearrange("p t c -> p c t"),
+                out=k_grouped[n, E_PASSES - 1][:, cols, :],
+                in0=k_sb[n, E_PASSES - 1][:, :, cols].rearrange("p t c -> p c t"),
                 scalar1=go[:],
                 scalar2=0.0,
                 op0=ALU.mult,
@@ -213,9 +215,12 @@ def tile_attentionlayer_pa_kernel(
             scales = work.tile([P, E_PASSES, TS], U8, align_bytes=64, name="k_scales")
             k_codes[n], k_scales[n] = codes, scales
 
+        def in_fours(n):
+            return n < BATCH - 1
+
         def project(n, passes=range(E_PASSES)):
             for ge in passes:
-                part = work.tile([P, PACK, TQ], F32, tag="rows_or_part", bufs=4)
+                part = work.tile([P, PACK * TQ], F32, tag="rows_or_part", bufs=4)
                 for t in range(PACK):
                     h_ps = psum_mx.tile([P, TQ], F32, tag="mx")
                     for gc in range(C_PASSES):
@@ -229,8 +234,14 @@ def tile_attentionlayer_pa_kernel(
                             stop=(gc == C_PASSES - 1),
                         )
                     m = PACK * ge + t
+                    if in_fours(n):
+                        dst = part[:].rearrange("p (c t r) -> p c t r", t=PACK, r=Q_TILES)[:, :, t, :]
+                        src = h_ps[:].rearrange("p (r c) -> p c r", r=Q_TILES)
+                    else:
+                        dst = part[:, TQ * t : TQ * t + TQ]
+                        src = h_ps[:]
                     nc.scalar.activation(
-                        out=part[:, t, :], in_=h_ps[:], func=ACT.Identity, bias=bias_s[:, m : m + 1], scale=SQRT_HALF
+                        out=dst, in_=src, func=ACT.Identity, bias=bias_s[:, m : m + 1], scale=SQRT_HALF
                     )
                 h_part[n, ge] = part
 
@@ -263,13 +274,18 @@ def tile_attentionlayer_pa_kernel(
             def add_embedding(i, ge):
                 hq, j, piece = piece_of_half(i)
                 in_half = slice(width * j, width * j + width)
+                result = piece[:, width * ge : width * ge + width, :]
+                embedding = te_ps[n, ge, hq][:, :, in_half]
+                if in_fours(n):
+                    part = h_part[n, ge][:].rearrange("p (c t r) -> p c t r", t=PACK, r=Q_TILES)
+                    result = result.rearrange("p (r c) t -> p c t r", c=P)
+                    embedding = embedding.rearrange("p t (r c) -> p c t r", c=P)
+                    part = part[:, :, :, 2 * hq : 2 * hq + 2]
+                else:
+                    part = h_part[n, ge][:].rearrange("p (t q) -> p q t", t=PACK)[:, width * i : width * i + width, :]
+                    embedding = embedding.rearrange("p t q -> p q t")
                 nc.vector.scalar_tensor_tensor(
-                    out=piece[:, width * ge : width * ge + width, :],
-                    in0=te_ps[n, ge, hq][:, :, in_half].rearrange("p t q -> p q t"),
-                    scalar=SQRT_HALF,
-                    in1=h_part[n, ge][:, :, width * i : width * i + width].rearrange("p t q -> p q t"),
-                    op0=ALU.mult,
-                    op1=ALU.add,
+                    out=result, in0=embedding, scalar=SQRT_HALF, in1=part, op0=ALU.mult, op1=ALU.add
                 )
 
             def quantise_piece(i):
@@ -430,6 +446,7 @@ def tile_attentionlayer_pa_kernel(
                 transpose_te(n + 1)
                 scores(n, vector_helps=False)
                 new_key_codes(n + 1)
+                regroup(n + 1, E_PASSES - 1, slice(GPSIMD_TO, TS), nc.vector.tensor_copy)
                 regroup(n + 1, 0, slice(0, SCALAR_FROM[n + 1]), nc.vector.tensor_copy)
                 quantise_pass(n + 1, E_PASSES - 1)
                 if n + 2 < BATCH:

import math
from contextlib import ExitStack

import concourse.mybir as mybir
from concourse.masks import make_identity

F32 = mybir.dt.float32
BF16 = mybir.dt.bfloat16
U32 = mybir.dt.uint32
U8 = mybir.dt.uint8
FP8X4 = mybir.dt.float8_e4m3fn_x4
ACT = mybir.ActivationFunctionType
ALU = mybir.AluOpType

P = 128
PACK = 4
K_PASS = P * PACK
N_MOVE = 512

BATCH, TQ, TS, C, E = 4, 512, 1024, 1024, 1024
C_PASSES = C // K_PASS
E_PASSES = E // K_PASS
E_TILES = E // P
Q_TILES = TQ // P
Q_HALF = TQ // 2
S_HALVES = TS // N_MOVE
SQRT_HALF = math.sqrt(0.5)
SCALAR_FROM = (512, 768, 768, 512)
GPSIMD_TO = 896
SCALAR_SQUARES = 576

FLOPS = 2 * BATCH * TQ * C * E + 2 * BATCH * TQ * E * TS


def tile_attentionlayer_pa_kernel(
    tc, x, target_embedding, encoder_keys, in_proj_v, in_proj_g, in_proj_b, out
):
    nc = tc.nc
    with ExitStack() as stack:
        stack.enter_context(tc.manual_schedule())
        const = stack.enter_context(tc.tile_pool(name="const", bufs=1))
        raw = stack.enter_context(tc.tile_pool(name="raw", bufs=10))
        work = stack.enter_context(tc.tile_pool(name="work", bufs=2))
        psum_t = stack.enter_context(tc.psum_pool(name="psum_t", bufs=4))
        psum_mx = stack.enter_context(tc.psum_pool(name="psum_mx", bufs=4))

        v_sb, w_rows, w_grouped = {}, {}, {}
        x_sb, k_sb, te_sb = {}, {}, {}
        x_grouped, x_codes, x_scales = {}, {}, {}
        k_grouped, k_codes, k_scales = {}, {}, {}
        h_part, te_ps, h_codes, h_scales, h_cols = {}, {}, {}, {}, {}

        def load_v(ge):
            v_tile = raw.tile([P, PACK, C], BF16, tag="raw")
            for t in range(PACK):
                row0 = K_PASS * ge + P * t
                nc.sync.dma_start(out=v_tile[:, t, :], in_=in_proj_v[row0 : row0 + P, :])
            v_sb[ge] = v_tile

        def load_x(n):
            x_tile = raw.tile([P, Q_TILES, C], BF16, tag="raw")
            nc.sync.dma_start(out=x_tile[:], in_=x[n].rearrange("(p r) c -> p r c", r=Q_TILES))
            x_sb[n] = x_tile

        def load_keys(n, ge):
            k_tile = raw.tile([P, PACK, TS], BF16, tag="raw")
            rows = encoder_keys[n][K_PASS * ge : K_PASS * ge + K_PASS, :]
            nc.sync.dma_start(out=k_tile[:], in_=rows.rearrange("(t p) s -> p t s", p=P))
            k_sb[n, ge] = k_tile

        def load_te(n):
            te_tile = raw.tile([P, Q_TILES, E], BF16, tag="raw")
            nc.sync.dma_start(out=te_tile[:], in_=target_embedding[n].rearrange("(p r) e -> p r e", r=Q_TILES))
            te_sb[n] = te_tile

        def sum_squares(ge, t):
            m = PACK * ge + t
            squares_s = work.tile([P, SCALAR_SQUARES], BF16, bufs=1)
            nc.scalar.activation(
                out=squares_s[:], in_=v_sb[ge][:, t, 0:SCALAR_SQUARES], func=ACT.Square, accum_out=sumsq_s[:, m : m + 1]
            )
            squares_v = work.tile([P, C - SCALAR_SQUARES], F32, bufs=1)
            nc.vector.scalar_tensor_tensor(
                out=squares_v[:],
                in0=v_sb[ge][:, t, SCALAR_SQUARES:C],
                scalar=1.0,
                in1=v_sb[ge][:, t, SCALAR_SQUARES:C],
                op0=ALU.mult,
                op1=ALU.mult,
                accum_out=sumsq_v[:, m : m + 1],
            )

        def add_sums(ge):
            cols = slice(PACK * ge, PACK * ge + PACK)
            nc.vector.tensor_add(out=sumsq[:, cols], in0=sumsq_s[:, cols], in1=sumsq_v[:, cols])

        def take_root(ge):
            cols = slice(PACK * ge, PACK * ge + PACK)
            nc.scalar.activation(out=norm[:, cols], in_=sumsq[:, cols], func=ACT.Sqrt)

        def invert_norm(ge):
            cols = slice(PACK * ge, PACK * ge + PACK)
            nc.vector.reciprocal(out=inv_norm[:, cols], in_=norm[:, cols])

        def new_w_rows(ge):
            rows = work.tile([P, PACK, C], BF16, tag="rows_or_part", bufs=4)
            w_rows[ge] = rows

        def scale_rows(ge, t):
            m = PACK * ge + t
            nc.vector.tensor_scalar(
                out=w_rows[ge][:, t, :],
                in0=v_sb[ge][:, t, :],
                scalar1=inv_norm[:, m : m + 1],
                scalar2=gain[:, m : m + 1],
                op0=ALU.mult,
                op1=ALU.mult,
            )

        def transpose_w(ge, pool, tag):
            grouped = work.tile([P, C_PASSES * K_PASS * PACK], BF16, align_bytes=64, tag="grouped", bufs=3, name="w_grouped")
            words = grouped[:].bitcast(F32).rearrange("p (g e u) -> p g e u", g=C_PASSES, u=2)
            for t in range(PACK):
                w_ps = pool.tile([P, 2 * C_PASSES, P], F32, tag=tag)
                for j in range(2 * C_PASSES):
                    nc.tensor.transpose(
                        w_ps[:, j, :], w_rows[ge][:, t, :].bitcast(F32)[:, P * j : P * j + P], ident_f32[:]
                    )
                dst = words[:, :, P * t : P * t + P, :]
                src = w_ps[:].rearrange("p (g u) e -> p g e u", u=2)
                if ge == 0 and t % 2 == 0:
                    nc.vector.tensor_copy(out=dst, in_=src)
                else:
                    nc.scalar.copy(out=dst, in_=src)
            w_grouped[ge] = grouped

        def quantise_w(ge):
            nc.vector.quantize_mx(
                out=w_codes[:, ge].rearrange("p g e -> p (g e)").bitcast(FP8X4),
                scales=w_scales[:, ge].rearrange("p g e -> p (g e)"),
                in_=w_grouped[ge][:],
            )

        def busy_matmuls(count, ge, t, pool, tag):
            unread = pool.tile([P, N_MOVE], F32, tag=tag)
            for j in range(count):
                nc.tensor.matmul(
                    unread[:], lhsT=v_sb[ge][:, t, 0:P], rhs=v_sb[ge][:, t, 0:N_MOVE], start=True, stop=True
                )

        def transpose_x(n, pool, tag):
            grouped = work.tile([P, C_PASSES * TQ * PACK], BF16, align_bytes=64, tag="grouped", bufs=3, name="x_grouped")
            words = grouped[:].bitcast(F32).rearrange("p (g q u) -> p g q u", g=C_PASSES, u=2)
            for r in range(Q_TILES):
                x_ps = pool.tile([P, 2 * C_PASSES, P], F32, tag=tag)
                for j in range(2 * C_PASSES):
                    nc.tensor.transpose(
                        x_ps[:, j, :], x_sb[n][:, r, :].bitcast(F32)[:, P * j : P * j + P], ident_f32[:]
                    )
                nc.scalar.copy(
                    out=words[:, :, P * r : P * r + P, :], in_=x_ps[:].rearrange("p (g u) q -> p g q u", u=2)
                )
            x_grouped[n] = grouped

        def quantise_x(n):
            codes = work.tile([P, C_PASSES, TQ], U32, align_bytes=64, name="x_codes")
            scales = work.tile([P, C_PASSES, TQ], U8, align_bytes=64, name="x_scales")
            nc.vector.quantize_mx(
                out=codes[:].rearrange("p g q -> p (g q)").bitcast(FP8X4),
                scales=scales[:].rearrange("p g q -> p (g q)"),
                in_=x_grouped[n][:],
            )
            x_codes[n], x_scales[n] = codes, scales

        def regrouped_views(grouped, n, ge, cols):
            return (
                grouped[:, cols, :].rearrange("p (c i) t -> p c t i", i=4),
                k_sb[n, ge][:, :, cols].rearrange("p t (c i) -> p c t i", i=4),
            )

        def new_last_pass(n):
            grouped = work.tile([P, TS, PACK], BF16, align_bytes=64, name="k_grouped_last")
            k_grouped[n, E_PASSES - 1] = grouped

        def regroup_on_gpsimd(n):
            go = work.tile([P, 1], F32)
            nc.vector.memset(go[:], 1.0)
            cols = slice(0, GPSIMD_TO)
            nc.gpsimd.tensor_scalar(
                out=k_grouped[n, E_PASSES - 1][:, cols, :],
                in0=k_sb[n, E_PASSES - 1][:, :, cols].rearrange("p t c -> p c t"),
                scalar1=go[:],
                scalar2=0.0,
                op0=ALU.mult,
                op1=ALU.add,
            )

        def new_first_pass(n):
            grouped = work.tile([P, TS, PACK], BF16, align_bytes=64, name="k_grouped_first", bufs=1)
            k_grouped[n, 0] = grouped

        def regroup(n, ge, cols, copy):
            dst, src = regrouped_views(k_grouped[n, ge], n, ge, cols)
            copy(out=dst, in_=src)

        def quantise_pass(n, ge):
            nc.vector.quantize_mx(
                out=k_codes[n][:, ge, :].bitcast(FP8X4),
                scales=k_scales[n][:, ge, :],
                in_=k_grouped[n, ge][:].rearrange("p s t -> p (s t)"),
            )

        def new_key_codes(n):
            codes = work.tile([P, E_PASSES, TS], U32, align_bytes=64, name="k_codes")
            scales = work.tile([P, E_PASSES, TS], U8, align_bytes=64, name="k_scales")
            k_codes[n], k_scales[n] = codes, scales

        def in_fours(n):
            return n < BATCH - 1

        def project(n, passes=range(E_PASSES)):
            for ge in passes:
                part = work.tile([P, PACK * TQ], F32, tag="rows_or_part", bufs=4)
                for t in range(PACK):
                    h_ps = psum_mx.tile([P, TQ], F32, tag="mx")
                    for gc in range(C_PASSES):
                        nc.tensor.matmul_mx(
                            out=h_ps[:],
                            lhsT=w_codes[:, ge, gc, P * t : P * t + P].bitcast(FP8X4),
                            lhsT_scale=w_scales[:, ge, gc, P * t : P * t + P],
                            rhs=x_codes[n][:, gc, :].bitcast(FP8X4),
                            rhs_scale=x_scales[n][:, gc, :],
                            start=(gc == 0),
                            stop=(gc == C_PASSES - 1),
                        )
                    m = PACK * ge + t
                    if in_fours(n):
                        dst = part[:].rearrange("p (c t r) -> p c t r", t=PACK, r=Q_TILES)[:, :, t, :]
                        src = h_ps[:].rearrange("p (r c) -> p c r", r=Q_TILES)
                    else:
                        dst = part[:, TQ * t : TQ * t + TQ]
                        src = h_ps[:]
                    nc.scalar.activation(
                        out=dst, in_=src, func=ACT.Identity, bias=bias_s[:, m : m + 1], scale=SQRT_HALF
                    )
                h_part[n, ge] = part

        def transpose_te(n):
            for hq in range(2):
                for ge in range(E_PASSES):
                    bank = psum_t.tile([P, PACK, Q_HALF], BF16, tag="tp", name="te_ps")
                    for t in range(PACK):
                        e0 = K_PASS * ge + P * t
                        for rr in range(2):
                            nc.tensor.transpose(
                                bank[:, t, P * rr : P * rr + P], te_sb[n][:, 2 * hq + rr, e0 : e0 + P], ident_bf[:]
                            )
                    te_ps[n, ge, hq] = bank

        def finish_h(n, pieces):
            width = TQ // pieces
            span = E_PASSES * width
            codes = work.tile([P, E_PASSES * TQ], U32, align_bytes=64, name="h_codes")
            scales = work.tile([P, E_PASSES * TQ], U8, align_bytes=64, name="h_scales")
            grouped = {}
            for hq in range(2):
                h_grouped = work.tile([P, E_PASSES * Q_HALF, PACK], BF16, align_bytes=64)
                grouped[hq] = h_grouped

            def piece_of_half(i):
                hq, j = divmod(i, pieces // 2)
                return hq, j, grouped[hq][:, span * j : span * j + span, :]

            def add_embedding(i, ge):
                hq, j, piece = piece_of_half(i)
                in_half = slice(width * j, width * j + width)
                result = piece[:, width * ge : width * ge + width, :]
                embedding = te_ps[n, ge, hq][:, :, in_half]
                if in_fours(n):
                    part = h_part[n, ge][:].rearrange("p (c t r) -> p c t r", t=PACK, r=Q_TILES)
                    result = result.rearrange("p (r c) t -> p c t r", c=P)
                    embedding = embedding.rearrange("p t (r c) -> p c t r", c=P)
                    part = part[:, :, :, 2 * hq : 2 * hq + 2]
                else:
                    part = h_part[n, ge][:].rearrange("p (t q) -> p q t", t=PACK)[:, width * i : width * i + width, :]
                    embedding = embedding.rearrange("p t q -> p q t")
                nc.vector.scalar_tensor_tensor(
                    out=result, in0=embedding, scalar=SQRT_HALF, in1=part, op0=ALU.mult, op1=ALU.add
                )

            def quantise_piece(i):
                hq, j, piece = piece_of_half(i)
                nc.vector.quantize_mx(
                    out=codes[:, span * i : span * i + span].bitcast(FP8X4),
                    scales=scales[:, span * i : span * i + span],
                    in_=piece.rearrange("p q t -> p (q t)"),
                )

            for i in range(pieces):
                add_embedding(i, 0)
                if pieces > 2 and i > 0:
                    quantise_piece(i - 1)
                add_embedding(i, 1)
                if pieces > 2 and i == 0:
                    quantise_pass(n, 0)
            if pieces == 2:
                quantise_piece(0)
            quantise_piece(pieces - 1)
            for r in range(Q_TILES):
                i, off = divmod(P * r, width)
                for ge in range(E_PASSES):
                    first = span * i + width * ge + off
                    h_cols[n, r, ge] = slice(first, first + P)
            h_codes[n], h_scales[n] = codes, scales

        def scores(n, vector_helps):
            out_rows = out[n].rearrange("(p r) s -> p r s", r=Q_TILES)
            for r in range(Q_TILES):
                o_sb = work.tile([P, TS], F32, bufs=4)
                for sh in range(S_HALVES):
                    s_cols = slice(N_MOVE * sh, N_MOVE * sh + N_MOVE)
                    o_ps = psum_mx.tile([P, N_MOVE], F32, tag="mx")
                    for ge in range(E_PASSES):
                        nc.tensor.matmul_mx(
                            out=o_ps[:],
                            lhsT=h_codes[n][:, h_cols[n, r, ge]].bitcast(FP8X4),
                            lhsT_scale=h_scales[n][:, h_cols[n, r, ge]],
                            rhs=k_codes[n][:, ge, s_cols].bitcast(FP8X4),
                            rhs_scale=k_scales[n][:, ge, s_cols],
                            start=(ge == 0),
                            stop=(ge == E_PASSES - 1),
                        )
                    if vector_helps and r >= 2 and sh == 1:
                        nc.vector.tensor_copy(out=o_sb[:, s_cols], in_=o_ps[:])
                    else:
                        nc.scalar.copy(out=o_sb[:, s_cols], in_=o_ps[:])
                    nc.sync.dma_start(out=out_rows[:, r, s_cols], in_=o_sb[:, s_cols])

        for ge in range(E_PASSES):
            load_v(ge)
        load_x(0)
        load_te(0)
        load_keys(0, 0)
        load_keys(0, 1)
        load_x(1)
        load_keys(1, 1)
        load_x(2)
        load_keys(1, 0)
        load_te(1)

        gb_rows = const.tile([P, P], BF16)
        nc.vector.memset(gb_rows[:], 0.0)
        nc.scalar.dma_start(out=gb_rows[0:E_TILES, :], in_=in_proj_g.rearrange("(m p) -> m p", p=P))
        nc.scalar.dma_start(out=gb_rows[E_TILES : 2 * E_TILES, :], in_=in_proj_b.rearrange("(m p) -> m p", p=P))

        one = const.tile([P, 1], F32)
        nc.vector.memset(one[:], 1.0)
        warm = const.tile([P, 1], F32)
        nc.scalar.activation(out=warm[:], in_=one[:], func=ACT.Sqrt)

        ident_bf = const.tile([P, P], BF16)
        make_identity(nc, ident_bf[:])
        ident_f32 = const.tile([P, P], F32)
        make_identity(nc, ident_f32[:])

        gb_ps = psum_t.tile([P, P], BF16, tag="tp")
        nc.tensor.transpose(gb_ps[:], gb_rows[:], ident_bf[:])
        gain = const.tile([P, E_TILES], F32)
        bias_s = const.tile([P, E_TILES], F32)

        w_codes = const.tile([P, E_PASSES, C_PASSES, K_PASS], U32, align_bytes=64)
        w_scales = const.tile([P, E_PASSES, C_PASSES, K_PASS], U8, align_bytes=64)

        sumsq_s = const.tile([P, E_TILES], F32)
        sumsq_v = const.tile([P, E_TILES], F32)
        sumsq = const.tile([P, E_TILES], F32)
        norm = const.tile([P, E_TILES], F32)
        inv_norm = const.tile([P, E_TILES], F32)

        for t in range(PACK):
            sum_squares(0, t)
        sum_squares(1, 0)
        nc.scalar.copy(out=gain[:], in_=gb_ps[:, 0:E_TILES])
        nc.scalar.mul(bias_s[:], gb_ps[:, E_TILES : 2 * E_TILES], SQRT_HALF)
        sum_squares(1, 1)
        add_sums(0)
        sum_squares(1, 2)
        take_root(0)
        sum_squares(1, 3)
        invert_norm(0)
        add_sums(1)
        take_root(1)
        new_w_rows(0)
        new_w_rows(1)
        scale_rows(0, 0)
        scale_rows(0, 1)
        invert_norm(1)
        scale_rows(0, 2)
        scale_rows(0, 3)
        for t in range(PACK):
            scale_rows(1, t)
        for t in range(PACK):
            busy_matmuls(2, 1, t, pool=psum_t, tag="tp")
        transpose_x(0, pool=psum_mx, tag="mx")
        busy_matmuls(2, 1, 3, pool=psum_t, tag="tp")
        transpose_w(0, pool=psum_t, tag="tp")
        quantise_x(0)
        quantise_w(0)
        busy_matmuls(2, 1, 3, pool=psum_mx, tag="mx")
        transpose_w(1, pool=psum_mx, tag="mx")
        busy_matmuls(2, 1, 3, pool=psum_t, tag="tp")
        transpose_te(0)
        quantise_w(1)
        new_first_pass(0)
        regroup(0, 0, slice(SCALAR_FROM[0], TS), nc.scalar.copy)
        project(0, passes=(0,))
        transpose_x(1, pool=psum_mx, tag="mx")
        project(0, passes=(1,))
        new_key_codes(0)
        regroup(0, 0, slice(0, SCALAR_FROM[0]), nc.vector.tensor_copy)
        new_last_pass(0)
        regroup(0, E_PASSES - 1, slice(0, TS), nc.vector.tensor_copy)
        quantise_pass(0, 0)
        quantise_x(1)

        for n in range(BATCH):
            if n + 2 < BATCH:
                load_keys(n + 2, 1)
                if n + 3 < BATCH:
                    load_x(n + 3)
                load_keys(n + 2, 0)
                load_te(n + 2)
            if n + 1 < BATCH:
                new_last_pass(n + 1)
                regroup_on_gpsimd(n + 1)
            finish_h(n, pieces=4 if n == BATCH - 1 else 2)
            if n == 0:
                quantise_pass(0, E_PASSES - 1)
            if n + 1 < BATCH:
                project(n + 1)
            if n + 2 < BATCH:
                transpose_x(n + 2, pool=psum_t, tag="tp")
            if n + 1 < BATCH:
                new_first_pass(n + 1)
                regroup(n + 1, 0, slice(SCALAR_FROM[n + 1], TS), nc.scalar.copy)
                transpose_te(n + 1)
                scores(n, vector_helps=False)
                new_key_codes(n + 1)
                regroup(n + 1, E_PASSES - 1, slice(GPSIMD_TO, TS), nc.vector.tensor_copy)
                regroup(n + 1, 0, slice(0, SCALAR_FROM[n + 1]), nc.vector.tensor_copy)
                quantise_pass(n + 1, E_PASSES - 1)
                if n + 2 < BATCH:
                    quantise_x(n + 2)
                    quantise_pass(n + 1, 0)
        scores(BATCH - 1, vector_helps=True)
